import numpy as np
import ml_dtypes


def mxq(x, axis, fmt="e4m3"):
    dtype, down = {"e4m3": (ml_dtypes.float8_e4m3fn, 7), "e5m2": (ml_dtypes.float8_e5m2, 14)}[fmt]
    v = np.moveaxis(np.asarray(x, np.float32).astype(ml_dtypes.bfloat16).astype(np.float64), axis, -1)
    blocks = v.reshape(v.shape[:-1] + (-1, 32))
    amax = np.abs(blocks).max(-1, keepdims=True)
    byte = np.maximum(np.where(amax > 0, np.frexp(amax)[1] - 1 + 127, 0) - down, 1)
    scale = np.exp2(byte - 127.0)
    codes = (blocks / scale).astype(np.float32).astype(dtype).astype(np.float64)
    return np.moveaxis((codes * scale).reshape(v.shape), -1, axis)


WIDE = False


def mx_kscale(k):
    if not WIDE:
        return np.ones(k)
    levels = np.array([10, -10, 5, -5, 0])
    if k % 512:
        return np.exp2(np.random.permutation(np.resize(levels, k // 32))).repeat(32)
    a = np.empty((k // 512, 16))
    for p in range(k // 512):
        a[p, :8] = np.random.permutation(np.resize(levels, 8))
        for g in range(8):
            far = levels[np.abs(levels - a[p, g]) >= 10]
            a[p, g + 8] = far[np.random.randint(len(far))]
    return np.exp2(a.ravel()).repeat(32)


BF16 = ml_dtypes.bfloat16


def bf(x):
    return np.asarray(x, np.float32).astype(BF16)


def f64(x):
    return np.asarray(x).astype(np.float64)


B, N, D, F1, F2, F3, G1, G2 = 4, 64, 512, 1024, 128, 512, 512, 512
ALPHA = 0.2


def lrelu(v):
    return np.maximum(v, ALPHA * v)


def setup_inputs():
    s, t = mx_kscale(D), mx_kscale(F1)
    ss = np.concatenate([s, s])
    return {"x": bf(np.random.standard_normal((B, N, D)) * s),
            "fe_w0": bf(np.random.standard_normal((D + D, F1)) / np.sqrt(D + D) / ss[:, None] * t),
            "fe_b0": bf(np.random.standard_normal(F1) * 0.3 * t),
            "fe_w1": bf(np.random.standard_normal((F1, F2)) * 1.4 / np.sqrt(F1) / t[:, None]),
            "fe_b1": bf(np.random.standard_normal(F2) * 0.3)}


def reference(x, fe_w0, fe_b0, fe_w1, fe_b1):
    xq = mxq(f64(x), 2, "e4m3")
    w0 = f64(fe_w0)
    u = xq @ mxq(w0[:D], 0, "e4m3")
    v = xq @ mxq(w0[D:], 0, "e4m3")
    e1 = lrelu(u[:, :, None, :] + v[:, None, :, :] + f64(fe_b0))
    return lrelu((mxq(e1, 3, "e4m3") @ mxq(f64(fe_w1), 0, "e4m3")) + f64(fe_b1))

@@ -1,0 +1,243 @@
+from contextlib import ExitStack
+
+import concourse.mybir as mybir
+from concourse.masks import make_identity
+
+BF16 = mybir.dt.bfloat16
+F32 = mybir.dt.float32
+U32 = mybir.dt.uint32
+U8 = mybir.dt.uint8
+FP8X4 = mybir.dt.float8_e4m3fn_x4
+ADD = mybir.AluOpType.add
+MULT = mybir.AluOpType.mult
+MAX = mybir.AluOpType.max
+IDENTITY = mybir.ActivationFunctionType.Identity
+
+P = 128
+PACK = 4
+K_PASS = P * PACK
+
+GRAPHS, NODES, D_IN, HIDDEN, D_OUT = 4, 64, 512, 1024, 128
+ROWS = GRAPHS * NODES
+ROW_TILES = ROWS // P
+HALVES = 2
+PASSES = HIDDEN // K_PASS
+FEATURE_TILES = HIDDEN // P
+ALPHA = 0.2
+
+I_PER_BLOCK = 8
+PAIRS = I_PER_BLOCK * NODES
+PAIR_TILES = PAIRS // P
+BLOCKS = ROWS // I_PER_BLOCK
+BLOCKS_PER_GRAPH = NODES // I_PER_BLOCK
+SUMS_AHEAD = 2
+
+FLOPS = 2 * HALVES * ROWS * D_IN * HIDDEN + 2 * ROWS * NODES * HIDDEN * D_OUT
+
+
+def side_by_side(copy, grouped, planes):
+    copy(
+        out=grouped.rearrange("p (g i) t -> p g t i", i=4),
+        in_=planes.rearrange("p t (g i) -> p g t i", i=4),
+    )
+
+
+def tile_graph_gan_pa_t_kernel(tc, x, fe_w0, fe_b0, fe_w1, fe_b1, out):
+    nc = tc.nc
+    x_rows = x.flatten_outer_dims()
+    out_rows = out.flatten_outer_dims()
+
+    with ExitStack() as stack:
+        keep = stack.enter_context(tc.tile_pool(name="keep", bufs=1))
+        sums = stack.enter_context(tc.tile_pool(name="sums", bufs=SUMS_AHEAD + 1))
+        hidden = stack.enter_context(tc.tile_pool(name="hidden", bufs=3))
+        results = stack.enter_context(tc.tile_pool(name="results", bufs=3))
+        psum_head = stack.enter_context(tc.psum_pool(name="psum_head", bufs=2))
+        psum_out = stack.enter_context(tc.psum_pool(name="psum_out", bufs=2))
+
+        identity_f32 = keep.tile([P, P], F32)
+        make_identity(nc, identity_f32[:])
+
+        x_sb = keep.tile([P, ROW_TILES, D_IN], BF16)
+        nc.sync.dma_start(out=x_sb[:], in_=x_rows.rearrange("(r p) d -> p r d", p=P))
+        b0_raw = keep.tile([P, PASSES, PACK], BF16)
+        nc.scalar.dma_start(out=b0_raw[:], in_=fe_b0.rearrange("(c p t) -> p c t", p=P, t=PACK))
+        b1_raw = keep.tile([P, 1], BF16)
+        nc.scalar.dma_start(out=b1_raw[:], in_=fe_b1.rearrange("(p o) -> p o", o=1))
+        w0_planes = keep.tile([P, HALVES, PACK, HIDDEN], BF16)
+        for c in range(PASSES):
+            f_cols = slice(c * K_PASS, (c + 1) * K_PASS)
+            for h in range(HALVES):
+                nc.sync.dma_start(
+                    out=w0_planes[:, h, :, f_cols],
+                    in_=fe_w0[h * D_IN : (h + 1) * D_IN, f_cols].rearrange(
+                        "(p t) f -> p t f", p=P
+                    ),
+                )
+        w1_planes = keep.tile([P, PASSES, PACK, D_OUT], BF16)
+        nc.sync.dma_start(
+            out=w1_planes[:], in_=fe_w1.rearrange("(c p t) n -> p c t n", t=PACK, p=P)
+        )
+
+        x_grouped = keep.tile([P, ROWS, PACK], BF16, align_bytes=64)
+        for r in range(ROW_TILES):
+            x_words = x_sb[:, r, :].bitcast(F32)
+            x_t = psum_head.tile([P, 2, P], F32, tag="transposed")
+            for e in range(2):
+                nc.tensor.transpose(x_t[:, e, :], x_words[:, e::2], identity_f32[:])
+            nc.vector.tensor_copy(
+                out=x_grouped[:, r * P : (r + 1) * P, :].rearrange("p r t -> p (r t)").bitcast(F32),
+                in_=x_t[:].rearrange("p e r -> p r e"),
+            )
+        x_codes = keep.tile([P, ROWS], U32, align_bytes=64)
+        x_scales = keep.tile([P, ROWS], U8, align_bytes=64)
+        nc.vector.quantize_mx(
+            out=x_codes[:].bitcast(FP8X4),
+            scales=x_scales[:],
+            in_=x_grouped[:].rearrange("p r t -> p (r t)"),
+        )
+
+        biases = keep.tile([P, FEATURE_TILES], F32)
+        nc.vector.tensor_copy(out=biases[:], in_=b0_raw[:].rearrange("p c t -> p (c t)"))
+        b1_tile = keep.tile([P, 1], F32)
+        nc.vector.tensor_copy(out=b1_tile[:], in_=b1_raw[:])
+        b1 = b1_tile[:]
+        b1_scaled = keep.tile([P, 1], F32)
+        nc.vector.tensor_scalar_mul(out=b1_scaled[:], in0=b1, scalar1=ALPHA)
+
+        w0_grouped = keep.tile([P, HALVES, HIDDEN, PACK], BF16, align_bytes=64)
+        w0_codes = keep.tile([P, HALVES, HIDDEN], U32, align_bytes=64)
+        w0_scales = keep.tile([P, HALVES, HIDDEN], U8, align_bytes=64)
+        u_b0 = keep.tile([P, FEATURE_TILES, ROWS], F32)
+        v = keep.tile([P, FEATURE_TILES, ROWS], F32)
+        for c in range(PASSES):
+            f_cols = slice(c * K_PASS, (c + 1) * K_PASS)
+            for h in range(HALVES):
+                nc.vector.tensor_copy(
+                    out=w0_grouped[:, h, f_cols, :].rearrange("p (t m) k -> p m t k", t=PACK),
+                    in_=w0_planes[:, h, :, f_cols].rearrange("p k (m t) -> p m t k", t=PACK),
+                )
+            for h in range(HALVES):
+                nc.vector.quantize_mx(
+                    out=w0_codes[:, h, f_cols].bitcast(FP8X4),
+                    scales=w0_scales[:, h, f_cols],
+                    in_=w0_grouped[:, h, f_cols, :].rearrange("p f t -> p (f t)"),
+                )
+            for ft in range(c * PACK, (c + 1) * PACK):
+                tile_cols = slice(ft * P, (ft + 1) * P)
+                uv = psum_head.tile([P, HALVES, ROWS], F32)
+                for h in range(HALVES):
+                    nc.tensor.matmul_mx(
+                        out=uv[:, h, :],
+                        lhsT=w0_codes[:, h, tile_cols].bitcast(FP8X4),
+                        lhsT_scale=w0_scales[:, h, tile_cols],
+                        rhs=x_codes[:].bitcast(FP8X4),
+                        rhs_scale=x_scales[:],
+                        start=True,
+                        stop=True,
+                    )
+                nc.scalar.activation(
+                    out=u_b0[:, ft, :], in_=uv[:, 0, :], func=IDENTITY, bias=biases[:, ft : ft + 1], scale=1.0
+                )
+                nc.vector.tensor_copy(out=v[:, ft, :], in_=uv[:, 1, :])
+
+        w1_grouped = keep.tile([P, PASSES, D_OUT, PACK], BF16, align_bytes=64)
+        for c in range(PASSES):
+            side_by_side(nc.scalar.copy, w1_grouped[:, c, :, :], w1_planes[:, c, :, :])
+        w1_codes = keep.tile([P, PASSES, D_OUT], U32, align_bytes=64)
+        w1_scales = keep.tile([P, PASSES, D_OUT], U8, align_bytes=64)
+        nc.vector.quantize_mx(
+            out=w1_codes[:].rearrange("p c n -> p (c n)").bitcast(FP8X4),
+            scales=w1_scales[:].rearrange("p c n -> p (c n)"),
+            in_=w1_grouped[:].rearrange("p c n t -> p (c n t)"),
+        )
+
+        def pair_sums(block):
+            graph = block // BLOCKS_PER_GRAPH
+            j_rows = slice(graph * NODES, (graph + 1) * NODES)
+            z = sums.tile([P, PASSES, PACK, PAIRS], F32)
+            for c in range(PASSES):
+                for t in range(PACK):
+                    ft = c * PACK + t
+                    for i in range(I_PER_BLOCK):
+                        i_row = block * I_PER_BLOCK + i
+                        nc.scalar.activation(
+                            out=z[:, c, t, i * NODES : (i + 1) * NODES],
+                            in_=v[:, ft, j_rows],
+                            func=IDENTITY,
+                            bias=u_b0[:, ft, i_row : i_row + 1],
+                            scale=1.0,
+                        )
+            return z
+
+        def first_leaky_relu(z):
+            e1 = hidden.tile([P, PASSES, PAIRS, PACK], BF16, align_bytes=64)
+            for c in range(PASSES):
+                z_words = z[:, c, :, :].rearrange("p t w -> p w t")
+                nc.vector.scalar_tensor_tensor(
+                    out=e1[:, c, :, :], in0=z_words, scalar=ALPHA, in1=z_words, op0=MULT, op1=MAX
+                )
+            return e1
+
+        def quantise(e1):
+            codes = hidden.tile([P, PASSES, PAIRS], U32, align_bytes=64)
+            scales = hidden.tile([P, PASSES, PAIRS], U8, align_bytes=64)
+            nc.vector.quantize_mx(
+                out=codes[:].rearrange("p c w -> p (c w)").bitcast(FP8X4),
+                scales=scales[:].rearrange("p c w -> p (c w)"),
+                in_=e1[:].rearrange("p c w t -> p (c w t)"),
+            )
+            return codes, scales
+
+        def second_product(codes, scales):
+            y_t = psum_out.tile([P, PAIRS], F32)
+            for c in range(PASSES):
+                nc.tensor.matmul_mx(
+                    out=y_t[:],
+                    lhsT=w1_codes[:, c, :].bitcast(FP8X4),
+                    lhsT_scale=w1_scales[:, c, :],
+                    rhs=codes[:, c, :].bitcast(FP8X4),
+                    rhs_scale=scales[:, c, :],
+                    start=(c == 0),
+                    stop=(c == PASSES - 1),
+                )
+            return y_t
+
+        def second_leaky_relu(y_t):
+            scaled = results.tile([P, PAIRS], F32)
+            nc.scalar.activation(out=scaled[:], in_=y_t[:], func=IDENTITY, bias=b1_scaled[:], scale=ALPHA)
+            out_t = results.tile([P, PAIRS], F32)
+            nc.vector.scalar_tensor_tensor(
+                out=out_t[:], in0=y_t[:], scalar=b1, in1=scaled[:], op0=ADD, op1=MAX
+            )
+            return out_t
+
+        def turn_and_store(block, out_t):
+            turned = psum_out.tile([P, PAIR_TILES, D_OUT], F32)
+            for g in range(PAIR_TILES):
+                nc.tensor.transpose(turned[:, g, :], out_t[:, g * P : (g + 1) * P], identity_f32[:])
+            result = results.tile([P, PAIR_TILES, D_OUT], F32)
+            nc.scalar.copy(out=result[:], in_=turned[:])
+            nc.sync.dma_start(
+                out=out_rows[block * PAIRS : (block + 1) * PAIRS, :].rearrange("(g p) n -> p g n", p=P),
+                in_=result[:],
+            )
+
+        sums_of = {}
+        product_of = {}
+        output_of = {}
+        for block in range(SUMS_AHEAD):
+            sums_of[block] = pair_sums(block)
+        for block in range(BLOCKS + 2):
+            if block < BLOCKS:
+                e1 = first_leaky_relu(sums_of[block])
+            if 1 <= block <= BLOCKS:
+                output_of[block - 1] = second_leaky_relu(product_of[block - 1])
+            if block < BLOCKS:
+                codes, scales = quantise(e1)
+            if block >= 2:
+                turn_and_store(block - 2, output_of[block - 2])
+            if block < BLOCKS:
+                product_of[block] = second_product(codes, scales)
+            if block + SUMS_AHEAD < BLOCKS:
+                sums_of[block + SUMS_AHEAD] = pair_sums(block + SUMS_AHEAD)

@@ -7,6 +7,7 @@ BF16 = mybir.dt.bfloat16
 F32 = mybir.dt.float32
 U32 = mybir.dt.uint32
 U8 = mybir.dt.uint8
+I32 = mybir.dt.int32
 FP8X4 = mybir.dt.float8_e4m3fn_x4
 ADD = mybir.AluOpType.add
 MULT = mybir.AluOpType.mult
@@ -30,6 +31,9 @@ PAIRS = I_PER_BLOCK * NODES
 PAIR_TILES = PAIRS // P
 BLOCKS = ROWS // I_PER_BLOCK
 BLOCKS_PER_GRAPH = NODES // I_PER_BLOCK
+J_HALF = 32
+HALF_PAIRS = I_PER_BLOCK * J_HALF
+J_HALVES = NODES // J_HALF
 SUMS_AHEAD = 2
 
 FLOPS = 2 * HALVES * ROWS * D_IN * HIDDEN + 2 * ROWS * NODES * HIDDEN * D_OUT
@@ -52,7 +56,8 @@ def tile_graph_gan_pa_t_kernel(tc, x, fe_w0, fe_b0, fe_w1, fe_b1, out):
         sums = stack.enter_context(tc.tile_pool(name="sums", bufs=SUMS_AHEAD + 1))
         hidden = stack.enter_context(tc.tile_pool(name="hidden", bufs=3))
         results = stack.enter_context(tc.tile_pool(name="results", bufs=3))
-        psum_head = stack.enter_context(tc.psum_pool(name="psum_head", bufs=2))
+        operands = stack.enter_context(tc.tile_pool(name="operands", bufs=2))
+        psum_z = stack.enter_context(tc.psum_pool(name="psum_z", bufs=4))
         psum_out = stack.enter_context(tc.psum_pool(name="psum_out", bufs=2))
 
         identity_f32 = keep.tile([P, P], F32)
@@ -79,23 +84,64 @@ def tile_graph_gan_pa_t_kernel(tc, x, fe_w0, fe_b0, fe_w1, fe_b1, out):
             out=w1_planes[:], in_=fe_w1.rearrange("(c p t) n -> p c t n", t=PACK, p=P)
         )
 
+        x_codes = keep.tile([P, ROWS], U32, align_bytes=64)
+        x_scales = keep.tile([P, ROWS], U8, align_bytes=64)
+        nc.gpsimd.memset(x_scales[:].bitcast(I32), 0)
         x_grouped = keep.tile([P, ROWS, PACK], BF16, align_bytes=64)
         for r in range(ROW_TILES):
             x_words = x_sb[:, r, :].bitcast(F32)
-            x_t = psum_head.tile([P, 2, P], F32, tag="transposed")
+            bank = psum_z.tile([P, PAIRS], F32, tag="z")
+            x_t = bank[:, 0 : 2 * P].rearrange("p (e r) -> p e r", e=2)
             for e in range(2):
                 nc.tensor.transpose(x_t[:, e, :], x_words[:, e::2], identity_f32[:])
             nc.vector.tensor_copy(
                 out=x_grouped[:, r * P : (r + 1) * P, :].rearrange("p r t -> p (r t)").bitcast(F32),
-                in_=x_t[:].rearrange("p e r -> p r e"),
+                in_=x_t.rearrange("p e r -> p r e"),
             )
-        x_codes = keep.tile([P, ROWS], U32, align_bytes=64)
-        x_scales = keep.tile([P, ROWS], U8, align_bytes=64)
         nc.vector.quantize_mx(
             out=x_codes[:].bitcast(FP8X4),
             scales=x_scales[:],
             in_=x_grouped[:].rearrange("p r t -> p (r t)"),
         )
+
+        def pair_operands(graph):
+            rows = slice(graph * NODES, (graph + 1) * NODES)
+            codes_i = operands.tile([P, NODES, J_HALF], U32, align_bytes=64)
+            codes_j = operands.tile([P, J_HALVES, I_PER_BLOCK, J_HALF], U32, align_bytes=64)
+            scales_i = operands.tile([P, NODES, J_HALF], U8, align_bytes=64)
+            scales_j = operands.tile([P, J_HALVES, I_PER_BLOCK, J_HALF], U8, align_bytes=64)
+            bytes_4 = operands.tile([P, NODES, 4], U8, align_bytes=64)
+            codes = x_codes[:, rows].bitcast(I32)
+            for n in range(4):
+                nc.vector.tensor_copy(out=bytes_4[:, :, n], in_=x_scales[:, rows])
+            nc.vector.tensor_copy(
+                out=codes_i[:].bitcast(I32), in_=codes.unsqueeze(2).to_broadcast([P, NODES, J_HALF])
+            )
+            words_4 = bytes_4[:].rearrange("p i n -> p (i n)").bitcast(I32)
+            nc.vector.tensor_copy(
+                out=scales_i[:].rearrange("p i j -> p (i j)").bitcast(I32).rearrange("p (i w) -> p i w", i=NODES),
+                in_=words_4.unsqueeze(2).to_broadcast([P, NODES, J_HALF // 4]),
+            )
+            words = x_scales[:, rows].bitcast(I32)
+            for half in range(J_HALVES):
+                nc.vector.tensor_copy(
+                    out=codes_j[:, half, :, :].bitcast(I32),
+                    in_=codes[:, half * J_HALF : (half + 1) * J_HALF]
+                    .unsqueeze(1)
+                    .to_broadcast([P, I_PER_BLOCK, J_HALF]),
+                )
+                nc.vector.tensor_copy(
+                    out=scales_j[:, half, :, :]
+                    .rearrange("p i j -> p (i j)")
+                    .bitcast(I32)
+                    .rearrange("p (i w) -> p i w", i=I_PER_BLOCK),
+                    in_=words[:, half * J_HALF // 4 : (half + 1) * J_HALF // 4]
+                    .unsqueeze(1)
+                    .to_broadcast([P, I_PER_BLOCK, J_HALF // 4]),
+                )
+            return codes_i, scales_i, codes_j, scales_j
+
+        operand_of = {0: pair_operands(0)}
 
         biases = keep.tile([P, FEATURE_TILES], F32)
         nc.vector.tensor_copy(out=biases[:], in_=b0_raw[:].rearrange("p c t -> p (c t)"))
@@ -108,12 +154,11 @@ def tile_graph_gan_pa_t_kernel(tc, x, fe_w0, fe_b0, fe_w1, fe_b1, out):
         w0_grouped = keep.tile([P, HALVES, HIDDEN, PACK], BF16, align_bytes=64)
         w0_codes = keep.tile([P, HALVES, HIDDEN], U32, align_bytes=64)
         w0_scales = keep.tile([P, HALVES, HIDDEN], U8, align_bytes=64)
-        u_b0 = keep.tile([P, FEATURE_TILES, ROWS], F32)
-        v = keep.tile([P, FEATURE_TILES, ROWS], F32)
         for c in range(PASSES):
             f_cols = slice(c * K_PASS, (c + 1) * K_PASS)
             for h in range(HALVES):
-                nc.vector.tensor_copy(
+                copy = nc.vector.tensor_copy if h == 0 else nc.scalar.copy
+                copy(
                     out=w0_grouped[:, h, f_cols, :].rearrange("p (t m) k -> p m t k", t=PACK),
                     in_=w0_planes[:, h, :, f_cols].rearrange("p k (m t) -> p m t k", t=PACK),
                 )
@@ -123,23 +168,6 @@ def tile_graph_gan_pa_t_kernel(tc, x, fe_w0, fe_b0, fe_w1, fe_b1, out):
                     scales=w0_scales[:, h, f_cols],
                     in_=w0_grouped[:, h, f_cols, :].rearrange("p f t -> p (f t)"),
                 )
-            for ft in range(c * PACK, (c + 1) * PACK):
-                tile_cols = slice(ft * P, (ft + 1) * P)
-                uv = psum_head.tile([P, HALVES, ROWS], F32)
-                for h in range(HALVES):
-                    nc.tensor.matmul_mx(
-                        out=uv[:, h, :],
-                        lhsT=w0_codes[:, h, tile_cols].bitcast(FP8X4),
-                        lhsT_scale=w0_scales[:, h, tile_cols],
-                        rhs=x_codes[:].bitcast(FP8X4),
-                        rhs_scale=x_scales[:],
-                        start=True,
-                        stop=True,
-                    )
-                nc.scalar.activation(
-                    out=u_b0[:, ft, :], in_=uv[:, 0, :], func=IDENTITY, bias=biases[:, ft : ft + 1], scale=1.0
-                )
-                nc.vector.tensor_copy(out=v[:, ft, :], in_=uv[:, 1, :])
 
         w1_grouped = keep.tile([P, PASSES, D_OUT, PACK], BF16, align_bytes=64)
         for c in range(PASSES):
@@ -152,22 +180,43 @@ def tile_graph_gan_pa_t_kernel(tc, x, fe_w0, fe_b0, fe_w1, fe_b1, out):
             in_=w1_grouped[:].rearrange("p c n t -> p (c n t)"),
         )
 
-        def pair_sums(block):
-            graph = block // BLOCKS_PER_GRAPH
-            j_rows = slice(graph * NODES, (graph + 1) * NODES)
+        def pair_sums(block, operand):
+            codes_i, scales_i, codes_j, scales_j = operand
+            i_first = block % BLOCKS_PER_GRAPH * I_PER_BLOCK
+            i_rows = slice(i_first, i_first + I_PER_BLOCK)
             z = sums.tile([P, PASSES, PACK, PAIRS], F32)
             for c in range(PASSES):
                 for t in range(PACK):
                     ft = c * PACK + t
-                    for i in range(I_PER_BLOCK):
-                        i_row = block * I_PER_BLOCK + i
-                        nc.scalar.activation(
-                            out=z[:, c, t, i * NODES : (i + 1) * NODES],
-                            in_=v[:, ft, j_rows],
-                            func=IDENTITY,
-                            bias=u_b0[:, ft, i_row : i_row + 1],
-                            scale=1.0,
+                    tile_cols = slice(ft * P, (ft + 1) * P)
+                    bank = psum_z.tile([P, PAIRS], F32, tag="z")
+                    for half in range(J_HALVES):
+                        half_bank = bank[:, half * HALF_PAIRS : (half + 1) * HALF_PAIRS]
+                        nc.tensor.matmul_mx(
+                            out=half_bank,
+                            lhsT=w0_codes[:, 0, tile_cols].bitcast(FP8X4),
+                            lhsT_scale=w0_scales[:, 0, tile_cols],
+                            rhs=codes_i[:, i_rows, :].rearrange("p i j -> p (i j)").bitcast(FP8X4),
+                            rhs_scale=scales_i[:, i_rows, :].rearrange("p i j -> p (i j)"),
+                            start=True,
+                            stop=False,
                         )
+                        nc.tensor.matmul_mx(
+                            out=half_bank,
+                            lhsT=w0_codes[:, 1, tile_cols].bitcast(FP8X4),
+                            lhsT_scale=w0_scales[:, 1, tile_cols],
+                            rhs=codes_j[:, half, :, :].rearrange("p i j -> p (i j)").bitcast(FP8X4),
+                            rhs_scale=scales_j[:, half, :, :].rearrange("p i j -> p (i j)"),
+                            start=False,
+                            stop=True,
+                        )
+                    nc.scalar.activation(
+                        out=z[:, c, t, :].rearrange("p (i h j) -> p i h j", i=I_PER_BLOCK, h=J_HALVES),
+                        in_=bank[:].rearrange("p (h i j) -> p i h j", h=J_HALVES, i=I_PER_BLOCK),
+                        func=IDENTITY,
+                        bias=biases[:, ft : ft + 1],
+                        scale=1.0,
+                    )
             return z
 
         def first_leaky_relu(z):
@@ -227,7 +276,7 @@ def tile_graph_gan_pa_t_kernel(tc, x, fe_w0, fe_b0, fe_w1, fe_b1, out):
         product_of = {}
         output_of = {}
         for block in range(SUMS_AHEAD):
-            sums_of[block] = pair_sums(block)
+            sums_of[block] = pair_sums(block, operand_of[0])
         for block in range(BLOCKS + 2):
             if block < BLOCKS:
                 e1 = first_leaky_relu(sums_of[block])
@@ -239,5 +288,9 @@ def tile_graph_gan_pa_t_kernel(tc, x, fe_w0, fe_b0, fe_w1, fe_b1, out):
                 turn_and_store(block - 2, output_of[block - 2])
             if block < BLOCKS:
                 product_of[block] = second_product(codes, scales)
-            if block + SUMS_AHEAD < BLOCKS:
-                sums_of[block + SUMS_AHEAD] = pair_sums(block + SUMS_AHEAD)
+            ahead = block + SUMS_AHEAD
+            if ahead < BLOCKS:
+                sums_of[ahead] = pair_sums(ahead, operand_of[ahead // BLOCKS_PER_GRAPH])
+            if ahead + 2 < BLOCKS and (ahead + 2) % BLOCKS_PER_GRAPH == 0:
+                next_graph = (ahead + 2) // BLOCKS_PER_GRAPH
+                operand_of[next_graph] = pair_operands(next_graph)

@@ -34,7 +34,7 @@ BLOCKS_PER_GRAPH = NODES // I_PER_BLOCK
 J_HALF = 32
 HALF_PAIRS = I_PER_BLOCK * J_HALF
 J_HALVES = NODES // J_HALF
-SUMS_AHEAD = 2
+SCALAR_ROWS = 2
 
 FLOPS = 2 * HALVES * ROWS * D_IN * HIDDEN + 2 * ROWS * NODES * HIDDEN * D_OUT
 
@@ -53,12 +53,14 @@ def tile_graph_gan_pa_t_kernel(tc, x, fe_w0, fe_b0, fe_w1, fe_b1, out):
 
     with ExitStack() as stack:
         keep = stack.enter_context(tc.tile_pool(name="keep", bufs=1))
-        sums = stack.enter_context(tc.tile_pool(name="sums", bufs=SUMS_AHEAD + 1))
+        lines = stack.enter_context(tc.tile_pool(name="lines", bufs=6))
+        planes = stack.enter_context(tc.tile_pool(name="planes", bufs=4))
         hidden = stack.enter_context(tc.tile_pool(name="hidden", bufs=3))
         results = stack.enter_context(tc.tile_pool(name="results", bufs=3))
         operands = stack.enter_context(tc.tile_pool(name="operands", bufs=2))
-        psum_z = stack.enter_context(tc.psum_pool(name="psum_z", bufs=4))
+        psum_z = stack.enter_context(tc.psum_pool(name="psum_z", bufs=5))
         psum_out = stack.enter_context(tc.psum_pool(name="psum_out", bufs=2))
+        psum_turn = stack.enter_context(tc.psum_pool(name="psum_turn", bufs=1))
 
         identity_f32 = keep.tile([P, P], F32)
         make_identity(nc, identity_f32[:])
@@ -145,6 +147,8 @@ def tile_graph_gan_pa_t_kernel(tc, x, fe_w0, fe_b0, fe_w1, fe_b1, out):
 
         biases = keep.tile([P, FEATURE_TILES], F32)
         nc.vector.tensor_copy(out=biases[:], in_=b0_raw[:].rearrange("p c t -> p (c t)"))
+        biases_scaled = keep.tile([P, FEATURE_TILES], F32)
+        nc.vector.tensor_scalar_mul(out=biases_scaled[:], in0=biases[:], scalar1=ALPHA)
         b1_tile = keep.tile([P, 1], F32)
         nc.vector.tensor_copy(out=b1_tile[:], in_=b1_raw[:])
         b1 = b1_tile[:]
@@ -180,53 +184,61 @@ def tile_graph_gan_pa_t_kernel(tc, x, fe_w0, fe_b0, fe_w1, fe_b1, out):
             in_=w1_grouped[:].rearrange("p c n t -> p (c n t)"),
         )
 
-        def pair_sums(block, operand):
+        def first_layer(block, c, operand):
             codes_i, scales_i, codes_j, scales_j = operand
             i_first = block % BLOCKS_PER_GRAPH * I_PER_BLOCK
             i_rows = slice(i_first, i_first + I_PER_BLOCK)
-            z = sums.tile([P, PASSES, PACK, PAIRS], F32)
-            for c in range(PASSES):
-                for t in range(PACK):
-                    ft = c * PACK + t
-                    tile_cols = slice(ft * P, (ft + 1) * P)
-                    bank = psum_z.tile([P, PAIRS], F32, tag="z")
-                    for half in range(J_HALVES):
-                        half_bank = bank[:, half * HALF_PAIRS : (half + 1) * HALF_PAIRS]
-                        nc.tensor.matmul_mx(
-                            out=half_bank,
-                            lhsT=w0_codes[:, 0, tile_cols].bitcast(FP8X4),
-                            lhsT_scale=w0_scales[:, 0, tile_cols],
-                            rhs=codes_i[:, i_rows, :].rearrange("p i j -> p (i j)").bitcast(FP8X4),
-                            rhs_scale=scales_i[:, i_rows, :].rearrange("p i j -> p (i j)"),
-                            start=True,
-                            stop=False,
-                        )
-                        nc.tensor.matmul_mx(
-                            out=half_bank,
-                            lhsT=w0_codes[:, 1, tile_cols].bitcast(FP8X4),
-                            lhsT_scale=w0_scales[:, 1, tile_cols],
-                            rhs=codes_j[:, half, :, :].rearrange("p i j -> p (i j)").bitcast(FP8X4),
-                            rhs_scale=scales_j[:, half, :, :].rearrange("p i j -> p (i j)"),
-                            start=False,
-                            stop=True,
-                        )
-                    nc.scalar.activation(
-                        out=z[:, c, t, :].rearrange("p (i h j) -> p i h j", i=I_PER_BLOCK, h=J_HALVES),
-                        in_=bank[:].rearrange("p (h i j) -> p i h j", h=J_HALVES, i=I_PER_BLOCK),
-                        func=IDENTITY,
-                        bias=biases[:, ft : ft + 1],
-                        scale=1.0,
+            e1_planes = planes.tile([P, PACK, PAIRS], BF16)
+            for t in range(PACK):
+                ft = c * PACK + t
+                tile_cols = slice(ft * P, (ft + 1) * P)
+                bank = psum_z.tile([P, PAIRS], F32, tag="z")
+                for half in range(J_HALVES):
+                    half_bank = bank[:, half * HALF_PAIRS : (half + 1) * HALF_PAIRS]
+                    nc.tensor.matmul_mx(
+                        out=half_bank,
+                        lhsT=w0_codes[:, 0, tile_cols].bitcast(FP8X4),
+                        lhsT_scale=w0_scales[:, 0, tile_cols],
+                        rhs=codes_i[:, i_rows, :].rearrange("p i j -> p (i j)").bitcast(FP8X4),
+                        rhs_scale=scales_i[:, i_rows, :].rearrange("p i j -> p (i j)"),
+                        start=True,
+                        stop=False,
                     )
-            return z
-
-        def first_leaky_relu(z):
-            e1 = hidden.tile([P, PASSES, PAIRS, PACK], BF16, align_bytes=64)
-            for c in range(PASSES):
-                z_words = z[:, c, :, :].rearrange("p t w -> p w t")
-                nc.vector.scalar_tensor_tensor(
-                    out=e1[:, c, :, :], in0=z_words, scalar=ALPHA, in1=z_words, op0=MULT, op1=MAX
+                    nc.tensor.matmul_mx(
+                        out=half_bank,
+                        lhsT=w0_codes[:, 1, tile_cols].bitcast(FP8X4),
+                        lhsT_scale=w0_scales[:, 1, tile_cols],
+                        rhs=codes_j[:, half, :, :].rearrange("p i j -> p (i j)").bitcast(FP8X4),
+                        rhs_scale=scales_j[:, half, :, :].rearrange("p i j -> p (i j)"),
+                        start=False,
+                        stop=True,
+                    )
+                low = lines.tile([P, PAIRS], F32)
+                nc.scalar.activation(
+                    out=low[:], in_=bank[:], func=IDENTITY, bias=biases_scaled[:, ft : ft + 1], scale=ALPHA
                 )
-            return e1
+                nc.vector.scalar_tensor_tensor(
+                    out=e1_planes[:, t, :],
+                    in0=bank[:],
+                    scalar=biases[:, ft : ft + 1],
+                    in1=low[:],
+                    op0=ADD,
+                    op1=MAX,
+                )
+            return e1_planes
+
+        def regroup(e1_planes, e1, c):
+            for half in range(J_HALVES):
+                source = e1_planes[:, :, half * HALF_PAIRS : (half + 1) * HALF_PAIRS].rearrange(
+                    "p t (i j) -> p i j t", i=I_PER_BLOCK
+                )
+                target = e1[:, c, :, :].rearrange("p (i h j) t -> p h i j t", i=I_PER_BLOCK, h=J_HALVES)[:, half]
+                cut = I_PER_BLOCK - (SCALAR_ROWS if half == J_HALVES - 1 else 0)
+                nc.gpsimd.tensor_scalar(
+                    out=target[:, :cut], in0=source[:, :cut], scalar1=1.0, scalar2=0.0, op0=MULT, op1=ADD
+                )
+                if cut < I_PER_BLOCK:
+                    nc.scalar.copy(out=target[:, cut:], in_=source[:, cut:])
 
         def quantise(e1):
             codes = hidden.tile([P, PASSES, PAIRS], U32, align_bytes=64)
@@ -262,7 +274,7 @@ def tile_graph_gan_pa_t_kernel(tc, x, fe_w0, fe_b0, fe_w1, fe_b1, out):
             return out_t
 
         def turn_and_store(block, out_t):
-            turned = psum_out.tile([P, PAIR_TILES, D_OUT], F32)
+            turned = psum_turn.tile([P, PAIR_TILES, D_OUT], F32)
             for g in range(PAIR_TILES):
                 nc.tensor.transpose(turned[:, g, :], out_t[:, g * P : (g + 1) * P], identity_f32[:])
             result = results.tile([P, PAIR_TILES, D_OUT], F32)
@@ -272,25 +284,19 @@ def tile_graph_gan_pa_t_kernel(tc, x, fe_w0, fe_b0, fe_w1, fe_b1, out):
                 in_=result[:],
             )
 
-        sums_of = {}
+        e1_of = {}
         product_of = {}
-        output_of = {}
-        for block in range(SUMS_AHEAD):
-            sums_of[block] = pair_sums(block, operand_of[0])
         for block in range(BLOCKS + 2):
             if block < BLOCKS:
-                e1 = first_leaky_relu(sums_of[block])
-            if 1 <= block <= BLOCKS:
-                output_of[block - 1] = second_leaky_relu(product_of[block - 1])
-            if block < BLOCKS:
-                codes, scales = quantise(e1)
+                operand = operand_of[block // BLOCKS_PER_GRAPH]
+                e1_of[block] = hidden.tile([P, PASSES, PAIRS, PACK], BF16, align_bytes=64, name="e1")
+                regroup(first_layer(block, 0, operand), e1_of[block], 0)
             if block >= 2:
-                turn_and_store(block - 2, output_of[block - 2])
+                turn_and_store(block - 2, second_leaky_relu(product_of[block - 2]))
             if block < BLOCKS:
-                product_of[block] = second_product(codes, scales)
-            ahead = block + SUMS_AHEAD
-            if ahead < BLOCKS:
-                sums_of[ahead] = pair_sums(ahead, operand_of[ahead // BLOCKS_PER_GRAPH])
-            if ahead + 2 < BLOCKS and (ahead + 2) % BLOCKS_PER_GRAPH == 0:
-                next_graph = (ahead + 2) // BLOCKS_PER_GRAPH
+                regroup(first_layer(block, 1, operand), e1_of[block], 1)
+            if 1 <= block <= BLOCKS:
+                product_of[block - 1] = second_product(*quantise(e1_of[block - 1]))
+            if block + 2 < BLOCKS and (block + 2) % BLOCKS_PER_GRAPH == 0:
+                next_graph = (block + 2) // BLOCKS_PER_GRAPH
                 operand_of[next_graph] = pair_operands(next_graph)

@@ -34,7 +34,7 @@ BLOCKS_PER_GRAPH = NODES // I_PER_BLOCK
 J_HALF = 32
 HALF_PAIRS = I_PER_BLOCK * J_HALF
 J_HALVES = NODES // J_HALF
-SCALAR_ROWS = 2
+SCALAR_WORDS = 64
 
 FLOPS = 2 * HALVES * ROWS * D_IN * HIDDEN + 2 * ROWS * NODES * HIDDEN * D_OUT
 
@@ -228,17 +228,16 @@ def tile_graph_gan_pa_t_kernel(tc, x, fe_w0, fe_b0, fe_w1, fe_b1, out):
             return e1_planes
 
         def regroup(e1_planes, e1, c):
-            for half in range(J_HALVES):
-                source = e1_planes[:, :, half * HALF_PAIRS : (half + 1) * HALF_PAIRS].rearrange(
-                    "p t (i j) -> p i j t", i=I_PER_BLOCK
-                )
-                target = e1[:, c, :, :].rearrange("p (i h j) t -> p h i j t", i=I_PER_BLOCK, h=J_HALVES)[:, half]
-                cut = I_PER_BLOCK - (SCALAR_ROWS if half == J_HALVES - 1 else 0)
-                nc.gpsimd.tensor_scalar(
-                    out=target[:, :cut], in0=source[:, :cut], scalar1=1.0, scalar2=0.0, op0=MULT, op1=ADD
-                )
-                if cut < I_PER_BLOCK:
-                    nc.scalar.copy(out=target[:, cut:], in_=source[:, cut:])
+            cut = PAIRS - SCALAR_WORDS
+            nc.gpsimd.tensor_scalar(
+                out=e1[:, c, :cut, :],
+                in0=e1_planes[:, :, :cut].rearrange("p t w -> p w t"),
+                scalar1=1.0,
+                scalar2=0.0,
+                op0=MULT,
+                op1=ADD,
+            )
+            side_by_side(nc.scalar.copy, e1[:, c, cut:, :], e1_planes[:, :, cut:])
 
         def quantise(e1):
             codes = hidden.tile([P, PASSES, PAIRS], U32, align_bytes=64)
@@ -268,9 +267,17 @@ def tile_graph_gan_pa_t_kernel(tc, x, fe_w0, fe_b0, fe_w1, fe_b1, out):
             scaled = results.tile([P, PAIRS], F32)
             nc.scalar.activation(out=scaled[:], in_=y_t[:], func=IDENTITY, bias=b1_scaled[:], scale=ALPHA)
             out_t = results.tile([P, PAIRS], F32)
-            nc.vector.scalar_tensor_tensor(
-                out=out_t[:], in0=y_t[:], scalar=b1, in1=scaled[:], op0=ADD, op1=MAX
-            )
+            ordered = out_t[:].rearrange("p (i h j) -> p h i j", i=I_PER_BLOCK, h=J_HALVES)
+            for half in range(J_HALVES):
+                cols = slice(half * HALF_PAIRS, (half + 1) * HALF_PAIRS)
+                nc.vector.scalar_tensor_tensor(
+                    out=ordered[:, half, :, :],
+                    in0=y_t[:, cols].rearrange("p (i j) -> p i j", i=I_PER_BLOCK),
+                    scalar=b1,
+                    in1=scaled[:, cols].rearrange("p (i j) -> p i j", i=I_PER_BLOCK),
+                    op0=ADD,
+                    op1=MAX,
+                )
             return out_t
 
         def turn_and_store(block, out_t):

@@ -62,22 +62,36 @@ def tile_graph_gan_pa_t_kernel(tc, x, fe_w0, fe_b0, fe_w1, fe_b1, out):
         psum_out = stack.enter_context(tc.psum_pool(name="psum_out", bufs=2))
         psum_turn = stack.enter_context(tc.psum_pool(name="psum_turn", bufs=1))
 
+        stack.enter_context(
+            tc.manual_schedule(
+                engines={
+                    mybir.EngineType.PE,
+                    mybir.EngineType.Activation,
+                    mybir.EngineType.DVE,
+                    mybir.EngineType.Pool,
+                }
+            )
+        )
+
         identity_f32 = keep.tile([P, P], F32)
         make_identity(nc, identity_f32[:])
+        warm = keep.tile([P, 1], F32)
+        nc.gpsimd.memset(warm[:], 0.0)
+        nc.scalar.activation(out=warm[:], in_=warm[:], func=IDENTITY, bias=0.0, scale=1.0)
 
         x_sb = keep.tile([P, ROW_TILES, D_IN], BF16)
-        nc.sync.dma_start(out=x_sb[:], in_=x_rows.rearrange("(r p) d -> p r d", p=P))
+        for r in range(ROW_TILES):
+            nc.sync.dma_start(out=x_sb[:, r, :], in_=x_rows[r * P : (r + 1) * P, :])
         b0_raw = keep.tile([P, PASSES, PACK], BF16)
         nc.scalar.dma_start(out=b0_raw[:], in_=fe_b0.rearrange("(c p t) -> p c t", p=P, t=PACK))
         b1_raw = keep.tile([P, 1], BF16)
         nc.scalar.dma_start(out=b1_raw[:], in_=fe_b1.rearrange("(p o) -> p o", o=1))
-        w0_planes = keep.tile([P, HALVES, PACK, HIDDEN], BF16)
+        w0_planes = keep.tile([P, PASSES, HALVES, PACK, K_PASS], BF16)
         for c in range(PASSES):
-            f_cols = slice(c * K_PASS, (c + 1) * K_PASS)
             for h in range(HALVES):
                 nc.sync.dma_start(
-                    out=w0_planes[:, h, :, f_cols],
-                    in_=fe_w0[h * D_IN : (h + 1) * D_IN, f_cols].rearrange(
+                    out=w0_planes[:, c, h, :, :],
+                    in_=fe_w0[h * D_IN : (h + 1) * D_IN, c * K_PASS : (c + 1) * K_PASS].rearrange(
                         "(p t) f -> p t f", p=P
                     ),
                 )
@@ -90,40 +104,34 @@ def tile_graph_gan_pa_t_kernel(tc, x, fe_w0, fe_b0, fe_w1, fe_b1, out):
         x_scales = keep.tile([P, ROWS], U8, align_bytes=64)
         nc.gpsimd.memset(x_scales[:].bitcast(I32), 0)
         x_grouped = keep.tile([P, ROWS, PACK], BF16, align_bytes=64)
-        for r in range(ROW_TILES):
+
+        def quantise_x(r):
+            tile_rows = slice(r * P, (r + 1) * P)
+            nc.vector.quantize_mx(
+                out=x_codes[:, tile_rows].bitcast(FP8X4),
+                scales=x_scales[:, tile_rows],
+                in_=x_grouped[:, tile_rows, :].rearrange("p r t -> p (r t)"),
+            )
+
+        def turn_x(r):
             x_words = x_sb[:, r, :].bitcast(F32)
             bank = psum_z.tile([P, PAIRS], F32, tag="z")
             x_t = bank[:, 0 : 2 * P].rearrange("p (e r) -> p e r", e=2)
             for e in range(2):
                 nc.tensor.transpose(x_t[:, e, :], x_words[:, e::2], identity_f32[:])
-            nc.vector.tensor_copy(
-                out=x_grouped[:, r * P : (r + 1) * P, :].rearrange("p r t -> p (r t)").bitcast(F32),
+            tile_rows = slice(r * P, (r + 1) * P)
+            nc.scalar.copy(
+                out=x_grouped[:, tile_rows, :].rearrange("p r t -> p (r t)").bitcast(F32),
                 in_=x_t.rearrange("p e r -> p r e"),
             )
-        nc.vector.quantize_mx(
-            out=x_codes[:].bitcast(FP8X4),
-            scales=x_scales[:],
-            in_=x_grouped[:].rearrange("p r t -> p (r t)"),
-        )
 
         def pair_operands(graph):
             rows = slice(graph * NODES, (graph + 1) * NODES)
             codes_i = operands.tile([P, NODES, J_HALF], U32, align_bytes=64)
-            codes_j = operands.tile([P, J_HALVES, I_PER_BLOCK, J_HALF], U32, align_bytes=64)
             scales_i = operands.tile([P, NODES, J_HALF], U8, align_bytes=64)
+            codes_j = operands.tile([P, J_HALVES, I_PER_BLOCK, J_HALF], U32, align_bytes=64)
             scales_j = operands.tile([P, J_HALVES, I_PER_BLOCK, J_HALF], U8, align_bytes=64)
-            bytes_4 = operands.tile([P, NODES, 4], U8, align_bytes=64)
             codes = x_codes[:, rows].bitcast(I32)
-            for n in range(4):
-                nc.vector.tensor_copy(out=bytes_4[:, :, n], in_=x_scales[:, rows])
-            nc.vector.tensor_copy(
-                out=codes_i[:].bitcast(I32), in_=codes.unsqueeze(2).to_broadcast([P, NODES, J_HALF])
-            )
-            words_4 = bytes_4[:].rearrange("p i n -> p (i n)").bitcast(I32)
-            nc.vector.tensor_copy(
-                out=scales_i[:].rearrange("p i j -> p (i j)").bitcast(I32).rearrange("p (i w) -> p i w", i=NODES),
-                in_=words_4.unsqueeze(2).to_broadcast([P, NODES, J_HALF // 4]),
-            )
             words = x_scales[:, rows].bitcast(I32)
             for half in range(J_HALVES):
                 nc.vector.tensor_copy(
@@ -143,89 +151,120 @@ def tile_graph_gan_pa_t_kernel(tc, x, fe_w0, fe_b0, fe_w1, fe_b1, out):
                 )
             return codes_i, scales_i, codes_j, scales_j
 
-        operand_of = {0: pair_operands(0)}
+        def fill_rows(graph, operand, first, last):
+            codes_i, scales_i = operand[:2]
+            count = last - first
+            rows = slice(graph * NODES + first, graph * NODES + last)
+            bytes_4 = operands.tile([P, NODES, 4], U8, align_bytes=64)
+            for n in range(4):
+                nc.vector.tensor_copy(out=bytes_4[:, :count, n], in_=x_scales[:, rows])
+            nc.vector.tensor_copy(
+                out=codes_i[:, first:last, :].bitcast(I32),
+                in_=x_codes[:, rows].bitcast(I32).unsqueeze(2).to_broadcast([P, count, J_HALF]),
+            )
+            words_4 = bytes_4[:].rearrange("p i n -> p (i n)").bitcast(I32)
+            nc.vector.tensor_copy(
+                out=scales_i[:, first:last, :]
+                .rearrange("p i j -> p (i j)")
+                .bitcast(I32)
+                .rearrange("p (i w) -> p i w", i=count),
+                in_=words_4[:, :count].unsqueeze(2).to_broadcast([P, count, J_HALF // 4]),
+            )
 
         biases = keep.tile([P, FEATURE_TILES], F32)
-        nc.vector.tensor_copy(out=biases[:], in_=b0_raw[:].rearrange("p c t -> p (c t)"))
+        nc.gpsimd.tensor_copy(out=biases[:], in_=b0_raw[:].rearrange("p c t -> p (c t)"))
         biases_scaled = keep.tile([P, FEATURE_TILES], F32)
-        nc.vector.tensor_scalar_mul(out=biases_scaled[:], in0=biases[:], scalar1=ALPHA)
+        nc.gpsimd.tensor_scalar(
+            out=biases_scaled[:], in0=biases[:], scalar1=ALPHA, scalar2=0.0, op0=MULT, op1=ADD
+        )
         b1_tile = keep.tile([P, 1], F32)
-        nc.vector.tensor_copy(out=b1_tile[:], in_=b1_raw[:])
+        nc.gpsimd.tensor_copy(out=b1_tile[:], in_=b1_raw[:])
         b1 = b1_tile[:]
         b1_scaled = keep.tile([P, 1], F32)
-        nc.vector.tensor_scalar_mul(out=b1_scaled[:], in0=b1, scalar1=ALPHA)
+        nc.gpsimd.tensor_scalar(out=b1_scaled[:], in0=b1, scalar1=ALPHA, scalar2=0.0, op0=MULT, op1=ADD)
 
         w0_grouped = keep.tile([P, HALVES, HIDDEN, PACK], BF16, align_bytes=64)
         w0_codes = keep.tile([P, HALVES, HIDDEN], U32, align_bytes=64)
         w0_scales = keep.tile([P, HALVES, HIDDEN], U8, align_bytes=64)
-        for c in range(PASSES):
+
+        def group_w0(copy, c, h):
             f_cols = slice(c * K_PASS, (c + 1) * K_PASS)
-            for h in range(HALVES):
-                copy = nc.vector.tensor_copy if h == 0 else nc.scalar.copy
-                copy(
-                    out=w0_grouped[:, h, f_cols, :].rearrange("p (t m) k -> p m t k", t=PACK),
-                    in_=w0_planes[:, h, :, f_cols].rearrange("p k (m t) -> p m t k", t=PACK),
-                )
-            for h in range(HALVES):
-                nc.vector.quantize_mx(
-                    out=w0_codes[:, h, f_cols].bitcast(FP8X4),
-                    scales=w0_scales[:, h, f_cols],
-                    in_=w0_grouped[:, h, f_cols, :].rearrange("p f t -> p (f t)"),
-                )
+            copy(
+                out=w0_grouped[:, h, f_cols, :].rearrange("p (t m) k -> p m t k", t=PACK),
+                in_=w0_planes[:, c, h, :, :].rearrange("p k (m t) -> p m t k", t=PACK),
+            )
+
+        def quantise_w0(c, h):
+            f_cols = slice(c * K_PASS, (c + 1) * K_PASS)
+            nc.vector.quantize_mx(
+                out=w0_codes[:, h, f_cols].bitcast(FP8X4),
+                scales=w0_scales[:, h, f_cols],
+                in_=w0_grouped[:, h, f_cols, :].rearrange("p f t -> p (f t)"),
+            )
+
+        for r in range(ROW_TILES):
+            turn_x(r)
+        group_w0(nc.vector.tensor_copy, 0, 0)
+        group_w0(nc.scalar.copy, 0, 1)
+        quantise_x(0)
+        operand_of = {0: pair_operands(0)}
+        fill_rows(0, operand_of[0], 0, I_PER_BLOCK)
+        quantise_w0(0, 0)
+        quantise_w0(0, 1)
+        group_w0(nc.vector.tensor_copy, 1, 0)
+        group_w0(nc.scalar.copy, 1, 1)
+        quantise_w0(1, 0)
+        quantise_w0(1, 1)
+        quantise_x(1)
 
         w1_grouped = keep.tile([P, PASSES, D_OUT, PACK], BF16, align_bytes=64)
-        for c in range(PASSES):
-            side_by_side(nc.scalar.copy, w1_grouped[:, c, :, :], w1_planes[:, c, :, :])
         w1_codes = keep.tile([P, PASSES, D_OUT], U32, align_bytes=64)
         w1_scales = keep.tile([P, PASSES, D_OUT], U8, align_bytes=64)
-        nc.vector.quantize_mx(
-            out=w1_codes[:].rearrange("p c n -> p (c n)").bitcast(FP8X4),
-            scales=w1_scales[:].rearrange("p c n -> p (c n)"),
-            in_=w1_grouped[:].rearrange("p c n t -> p (c n t)"),
-        )
 
-        def first_layer(block, c, operand):
+        def group_w1():
+            for c in range(PASSES):
+                side_by_side(nc.scalar.copy, w1_grouped[:, c, :, :], w1_planes[:, c, :, :])
+
+        def quantise_w1():
+            nc.vector.quantize_mx(
+                out=w1_codes[:].rearrange("p c n -> p (c n)").bitcast(FP8X4),
+                scales=w1_scales[:].rearrange("p c n -> p (c n)"),
+                in_=w1_grouped[:].rearrange("p c n t -> p (c n t)"),
+            )
+
+        def first_layer(block, ft, operand, plane):
             codes_i, scales_i, codes_j, scales_j = operand
             i_first = block % BLOCKS_PER_GRAPH * I_PER_BLOCK
             i_rows = slice(i_first, i_first + I_PER_BLOCK)
-            e1_planes = planes.tile([P, PACK, PAIRS], BF16)
-            for t in range(PACK):
-                ft = c * PACK + t
-                tile_cols = slice(ft * P, (ft + 1) * P)
-                bank = psum_z.tile([P, PAIRS], F32, tag="z")
-                for half in range(J_HALVES):
-                    half_bank = bank[:, half * HALF_PAIRS : (half + 1) * HALF_PAIRS]
-                    nc.tensor.matmul_mx(
-                        out=half_bank,
-                        lhsT=w0_codes[:, 0, tile_cols].bitcast(FP8X4),
-                        lhsT_scale=w0_scales[:, 0, tile_cols],
-                        rhs=codes_i[:, i_rows, :].rearrange("p i j -> p (i j)").bitcast(FP8X4),
-                        rhs_scale=scales_i[:, i_rows, :].rearrange("p i j -> p (i j)"),
-                        start=True,
-                        stop=False,
-                    )
-                    nc.tensor.matmul_mx(
-                        out=half_bank,
-                        lhsT=w0_codes[:, 1, tile_cols].bitcast(FP8X4),
-                        lhsT_scale=w0_scales[:, 1, tile_cols],
-                        rhs=codes_j[:, half, :, :].rearrange("p i j -> p (i j)").bitcast(FP8X4),
-                        rhs_scale=scales_j[:, half, :, :].rearrange("p i j -> p (i j)"),
-                        start=False,
-                        stop=True,
-                    )
-                low = lines.tile([P, PAIRS], F32)
-                nc.scalar.activation(
-                    out=low[:], in_=bank[:], func=IDENTITY, bias=biases_scaled[:, ft : ft + 1], scale=ALPHA
+            tile_cols = slice(ft * P, (ft + 1) * P)
+            bank = psum_z.tile([P, PAIRS], F32, tag="z")
+            for half in range(J_HALVES):
+                half_bank = bank[:, half * HALF_PAIRS : (half + 1) * HALF_PAIRS]
+                nc.tensor.matmul_mx(
+                    out=half_bank,
+                    lhsT=w0_codes[:, 0, tile_cols].bitcast(FP8X4),
+                    lhsT_scale=w0_scales[:, 0, tile_cols],
+                    rhs=codes_i[:, i_rows, :].rearrange("p i j -> p (i j)").bitcast(FP8X4),
+                    rhs_scale=scales_i[:, i_rows, :].rearrange("p i j -> p (i j)"),
+                    start=True,
+                    stop=False,
                 )
-                nc.vector.scalar_tensor_tensor(
-                    out=e1_planes[:, t, :],
-                    in0=bank[:],
-                    scalar=biases[:, ft : ft + 1],
-                    in1=low[:],
-                    op0=ADD,
-                    op1=MAX,
+                nc.tensor.matmul_mx(
+                    out=half_bank,
+                    lhsT=w0_codes[:, 1, tile_cols].bitcast(FP8X4),
+                    lhsT_scale=w0_scales[:, 1, tile_cols],
+                    rhs=codes_j[:, half, :, :].rearrange("p i j -> p (i j)").bitcast(FP8X4),
+                    rhs_scale=scales_j[:, half, :, :].rearrange("p i j -> p (i j)"),
+                    start=False,
+                    stop=True,
                 )
-            return e1_planes
+            low = lines.tile([P, PAIRS], F32)
+            nc.scalar.activation(
+                out=low[:], in_=bank[:], func=IDENTITY, bias=biases_scaled[:, ft : ft + 1], scale=ALPHA
+            )
+            nc.vector.scalar_tensor_tensor(
+                out=plane, in0=bank[:], scalar=biases[:, ft : ft + 1], in1=low[:], op0=ADD, op1=MAX
+            )
 
         def regroup(e1_planes, e1, c):
             cut = PAIRS - SCALAR_WORDS
@@ -237,6 +276,9 @@ def tile_graph_gan_pa_t_kernel(tc, x, fe_w0, fe_b0, fe_w1, fe_b1, out):
                 op0=MULT,
                 op1=ADD,
             )
+
+        def regroup_rest(e1_planes, e1, c):
+            cut = PAIRS - SCALAR_WORDS
             side_by_side(nc.scalar.copy, e1[:, c, cut:, :], e1_planes[:, :, cut:])
 
         def quantise(e1):
@@ -280,10 +322,13 @@ def tile_graph_gan_pa_t_kernel(tc, x, fe_w0, fe_b0, fe_w1, fe_b1, out):
                 )
             return out_t
 
-        def turn_and_store(block, out_t):
+        def turn(out_t):
             turned = psum_turn.tile([P, PAIR_TILES, D_OUT], F32)
             for g in range(PAIR_TILES):
                 nc.tensor.transpose(turned[:, g, :], out_t[:, g * P : (g + 1) * P], identity_f32[:])
+            return turned
+
+        def store(block, turned):
             result = results.tile([P, PAIR_TILES, D_OUT], F32)
             nc.scalar.copy(out=result[:], in_=turned[:])
             nc.sync.dma_start(
@@ -291,19 +336,40 @@ def tile_graph_gan_pa_t_kernel(tc, x, fe_w0, fe_b0, fe_w1, fe_b1, out):
                 in_=result[:],
             )
 
-        e1_of = {}
-        product_of = {}
-        for block in range(BLOCKS + 2):
-            if block < BLOCKS:
-                operand = operand_of[block // BLOCKS_PER_GRAPH]
-                e1_of[block] = hidden.tile([P, PASSES, PAIRS, PACK], BF16, align_bytes=64, name="e1")
-                regroup(first_layer(block, 0, operand), e1_of[block], 0)
-            if block >= 2:
-                turn_and_store(block - 2, second_leaky_relu(product_of[block - 2]))
-            if block < BLOCKS:
-                regroup(first_layer(block, 1, operand), e1_of[block], 1)
-            if 1 <= block <= BLOCKS:
-                product_of[block - 1] = second_product(*quantise(e1_of[block - 1]))
-            if block + 2 < BLOCKS and (block + 2) % BLOCKS_PER_GRAPH == 0:
-                next_graph = (block + 2) // BLOCKS_PER_GRAPH
+        e1_of, planes_of, quantised_of, product_of, output_of, turned_of = {}, {}, {}, {}, {}, {}
+        for r in range(BLOCKS + 3):
+            operand = operand_of[min(r, BLOCKS - 1) // BLOCKS_PER_GRAPH]
+            for ft in range(FEATURE_TILES):
+                c, t = divmod(ft, PACK)
+                if r < BLOCKS:
+                    if ft == 0:
+                        e1_of[r] = hidden.tile([P, PASSES, PAIRS, PACK], BF16, align_bytes=64, name="e1")
+                    if t == 0:
+                        planes_of[r, c] = planes.tile([P, PACK, PAIRS], BF16, name="e1_planes")
+                    first_layer(r, ft, operand, planes_of[r, c][:, t, :])
+                    if t == PACK - 1:
+                        regroup(planes_of[r, c], e1_of[r], c)
+                if ft == 2 and 1 <= r <= BLOCKS:
+                    regroup_rest(planes_of[r - 1, 1], e1_of[r - 1], 1)
+                if ft == 2 and 3 <= r:
+                    turned_of[r - 3] = turn(output_of[r - 3])
+                if ft == 4 and 2 <= r < BLOCKS + 2:
+                    product_of[r - 2] = second_product(*quantised_of[r - 2])
+                if ft == 4 and 3 <= r:
+                    store(r - 3, turned_of[r - 3])
+                if ft == 6 and r < BLOCKS:
+                    regroup_rest(planes_of[r, 0], e1_of[r], 0)
+                if ft == 6 and 2 <= r < BLOCKS + 2:
+                    output_of[r - 2] = second_leaky_relu(product_of[r - 2])
+                if ft == 7 and 1 <= r <= BLOCKS:
+                    quantised_of[r - 1] = quantise(e1_of[r - 1])
+                if r == 0 and ft == 3:
+                    fill_rows(0, operand, I_PER_BLOCK, NODES)
+                if r == 0 and ft == 4:
+                    group_w1()
+                if r == 0 and ft == 7:
+                    quantise_w1()
+            if r + 2 < BLOCKS and (r + 2) % BLOCKS_PER_GRAPH == 0:
+                next_graph = (r + 2) // BLOCKS_PER_GRAPH
                 operand_of[next_graph] = pair_operands(next_graph)
+                fill_rows(next_graph, operand_of[next_graph], 0, NODES)

@@ -53,7 +53,7 @@ def tile_graph_gan_pa_t_kernel(tc, x, fe_w0, fe_b0, fe_w1, fe_b1, out):
 
     with ExitStack() as stack:
         keep = stack.enter_context(tc.tile_pool(name="keep", bufs=1))
-        lines = stack.enter_context(tc.tile_pool(name="lines", bufs=6))
+        lines = stack.enter_context(tc.tile_pool(name="lines", bufs=8))
         planes = stack.enter_context(tc.tile_pool(name="planes", bufs=4))
         hidden = stack.enter_context(tc.tile_pool(name="hidden", bufs=3))
         results = stack.enter_context(tc.tile_pool(name="results", bufs=3))
@@ -305,9 +305,12 @@ def tile_graph_gan_pa_t_kernel(tc, x, fe_w0, fe_b0, fe_w1, fe_b1, out):
                 )
             return y_t
 
-        def second_leaky_relu(y_t):
+        def scale_product(y_t):
             scaled = results.tile([P, PAIRS], F32)
             nc.scalar.activation(out=scaled[:], in_=y_t[:], func=IDENTITY, bias=b1_scaled[:], scale=ALPHA)
+            return y_t, scaled
+
+        def second_leaky_relu(y_t, scaled):
             out_t = results.tile([P, PAIRS], F32)
             ordered = out_t[:].rearrange("p (i h j) -> p h i j", i=I_PER_BLOCK, h=J_HALVES)
             for half in range(J_HALVES):
@@ -336,8 +339,9 @@ def tile_graph_gan_pa_t_kernel(tc, x, fe_w0, fe_b0, fe_w1, fe_b1, out):
                 in_=result[:],
             )
 
-        e1_of, planes_of, quantised_of, product_of, output_of, turned_of = {}, {}, {}, {}, {}, {}
-        for r in range(BLOCKS + 3):
+        e1_of, planes_of, quantised_of, product_of = {}, {}, {}, {}
+        scaled_of, output_of, turned_of = {}, {}, {}
+        for r in range(BLOCKS + 4):
             operand = operand_of[min(r, BLOCKS - 1) // BLOCKS_PER_GRAPH]
             for ft in range(FEATURE_TILES):
                 c, t = divmod(ft, PACK)
@@ -349,18 +353,20 @@ def tile_graph_gan_pa_t_kernel(tc, x, fe_w0, fe_b0, fe_w1, fe_b1, out):
                     first_layer(r, ft, operand, planes_of[r, c][:, t, :])
                     if t == PACK - 1:
                         regroup(planes_of[r, c], e1_of[r], c)
-                if ft == 2 and 1 <= r <= BLOCKS:
+                if ft == 0 and 3 <= r < BLOCKS + 3:
+                    scaled_of[r - 3] = scale_product(product_of[r - 3])
+                if ft == 0 and 4 <= r:
+                    turned_of[r - 4] = turn(output_of[r - 4])
+                if ft == 3 and 1 <= r <= BLOCKS:
                     regroup_rest(planes_of[r - 1, 1], e1_of[r - 1], 1)
-                if ft == 2 and 3 <= r:
-                    turned_of[r - 3] = turn(output_of[r - 3])
+                if ft == 3 and 3 <= r < BLOCKS + 3:
+                    output_of[r - 3] = second_leaky_relu(*scaled_of[r - 3])
+                if ft == 3 and 4 <= r:
+                    store(r - 4, turned_of[r - 4])
                 if ft == 4 and 2 <= r < BLOCKS + 2:
                     product_of[r - 2] = second_product(*quantised_of[r - 2])
-                if ft == 4 and 3 <= r:
-                    store(r - 3, turned_of[r - 3])
-                if ft == 6 and r < BLOCKS:
+                if ft == 7 and r < BLOCKS:
                     regroup_rest(planes_of[r, 0], e1_of[r], 0)
-                if ft == 6 and 2 <= r < BLOCKS + 2:
-                    output_of[r - 2] = second_leaky_relu(product_of[r - 2])
                 if ft == 7 and 1 <= r <= BLOCKS:
                     quantised_of[r - 1] = quantise(e1_of[r - 1])
                 if r == 0 and ft == 3:

@@ -35,6 +35,7 @@ J_HALF = 32
 HALF_PAIRS = I_PER_BLOCK * J_HALF
 J_HALVES = NODES // J_HALF
 SCALAR_WORDS = 64
+LAST_SCALAR_WORDS = 288
 
 FLOPS = 2 * HALVES * ROWS * D_IN * HIDDEN + 2 * ROWS * NODES * HIDDEN * D_OUT
 
@@ -75,6 +76,10 @@ def tile_graph_gan_pa_t_kernel(tc, x, fe_w0, fe_b0, fe_w1, fe_b1, out):
 
         identity_f32 = keep.tile([P, P], F32)
         make_identity(nc, identity_f32[:])
+        b0_raw = keep.tile([P, PASSES, PACK], BF16)
+        nc.scalar.dma_start(out=b0_raw[:], in_=fe_b0.rearrange("(c p t) -> p c t", p=P, t=PACK))
+        b1_raw = keep.tile([P, 1], BF16)
+        nc.scalar.dma_start(out=b1_raw[:], in_=fe_b1.rearrange("(p o) -> p o", o=1))
         warm = keep.tile([P, 1], F32)
         nc.gpsimd.memset(warm[:], 0.0)
         nc.scalar.activation(out=warm[:], in_=warm[:], func=IDENTITY, bias=0.0, scale=1.0)
@@ -82,10 +87,6 @@ def tile_graph_gan_pa_t_kernel(tc, x, fe_w0, fe_b0, fe_w1, fe_b1, out):
         x_sb = keep.tile([P, ROW_TILES, D_IN], BF16)
         for r in range(ROW_TILES):
             nc.sync.dma_start(out=x_sb[:, r, :], in_=x_rows[r * P : (r + 1) * P, :])
-        b0_raw = keep.tile([P, PASSES, PACK], BF16)
-        nc.scalar.dma_start(out=b0_raw[:], in_=fe_b0.rearrange("(c p t) -> p c t", p=P, t=PACK))
-        b1_raw = keep.tile([P, 1], BF16)
-        nc.scalar.dma_start(out=b1_raw[:], in_=fe_b1.rearrange("(p o) -> p o", o=1))
         w0_planes = keep.tile([P, PASSES, HALVES, PACK, K_PASS], BF16)
         for c in range(PASSES):
             for h in range(HALVES):
@@ -281,18 +282,28 @@ def tile_graph_gan_pa_t_kernel(tc, x, fe_w0, fe_b0, fe_w1, fe_b1, out):
             cut = PAIRS - SCALAR_WORDS
             side_by_side(nc.scalar.copy, e1[:, c, cut:, :], e1_planes[:, :, cut:])
 
-        def quantise(e1):
+        def regroup_last(e1_planes, e1, c):
+            cut = PAIRS - LAST_SCALAR_WORDS
+            side_by_side(nc.scalar.copy, e1[:, c, cut:, :], e1_planes[:, :, cut:])
+            nc.vector.tensor_copy(
+                out=e1[:, c, :cut, :], in_=e1_planes[:, :, :cut].rearrange("p t w -> p w t")
+            )
+
+        def quantised_tiles():
             codes = hidden.tile([P, PASSES, PAIRS], U32, align_bytes=64)
             scales = hidden.tile([P, PASSES, PAIRS], U8, align_bytes=64)
-            nc.vector.quantize_mx(
-                out=codes[:].rearrange("p c w -> p (c w)").bitcast(FP8X4),
-                scales=scales[:].rearrange("p c w -> p (c w)"),
-                in_=e1[:].rearrange("p c w t -> p (c w t)"),
-            )
             return codes, scales
 
-        def second_product(codes, scales):
-            y_t = psum_out.tile([P, PAIRS], F32)
+        def quantise(e1, quantised, run):
+            codes, scales = quantised
+            nc.vector.quantize_mx(
+                out=codes[:, run, :].rearrange("p c w -> p (c w)").bitcast(FP8X4),
+                scales=scales[:, run, :].rearrange("p c w -> p (c w)"),
+                in_=e1[:, run, :, :].rearrange("p c w t -> p (c w t)"),
+            )
+
+        def second_product(codes, scales, pool=psum_out, tag="y"):
+            y_t = pool.tile([P, PAIRS], F32, tag=tag)
             for c in range(PASSES):
                 nc.tensor.matmul_mx(
                     out=y_t[:],
@@ -305,9 +316,14 @@ def tile_graph_gan_pa_t_kernel(tc, x, fe_w0, fe_b0, fe_w1, fe_b1, out):
                 )
             return y_t
 
-        def scale_product(y_t):
+        def scale_product(y_t, pieces=1):
             scaled = results.tile([P, PAIRS], F32)
-            nc.scalar.activation(out=scaled[:], in_=y_t[:], func=IDENTITY, bias=b1_scaled[:], scale=ALPHA)
+            width = PAIRS // pieces
+            for first in range(0, PAIRS, width):
+                columns = slice(first, first + width)
+                nc.scalar.activation(
+                    out=scaled[:, columns], in_=y_t[:, columns], func=IDENTITY, bias=b1_scaled[:], scale=ALPHA
+                )
             return y_t, scaled
 
         def second_leaky_relu(y_t, scaled):
@@ -325,50 +341,57 @@ def tile_graph_gan_pa_t_kernel(tc, x, fe_w0, fe_b0, fe_w1, fe_b1, out):
                 )
             return out_t
 
-        def turn(out_t):
-            turned = psum_turn.tile([P, PAIR_TILES, D_OUT], F32)
+        def turn(out_t, pool=psum_turn, tag="turned"):
+            turned = pool.tile([P, PAIRS], F32, tag=tag)
             for g in range(PAIR_TILES):
-                nc.tensor.transpose(turned[:, g, :], out_t[:, g * P : (g + 1) * P], identity_f32[:])
+                columns = slice(g * P, (g + 1) * P)
+                nc.tensor.transpose(turned[:, columns], out_t[:, columns], identity_f32[:])
             return turned
 
-        def store(block, turned):
+        def store(block, turned, pieces=1):
             result = results.tile([P, PAIR_TILES, D_OUT], F32)
-            nc.scalar.copy(out=result[:], in_=turned[:])
-            nc.sync.dma_start(
-                out=out_rows[block * PAIRS : (block + 1) * PAIRS, :].rearrange("(g p) n -> p g n", p=P),
-                in_=result[:],
-            )
+            tiles = PAIR_TILES // pieces
+            for g in range(0, PAIR_TILES, tiles):
+                nc.scalar.copy(
+                    out=result[:, g : g + tiles, :].rearrange("p g n -> p (g n)"),
+                    in_=turned[:, g * P : (g + tiles) * P],
+                )
+                first = block * PAIRS + g * P
+                nc.sync.dma_start(
+                    out=out_rows[first : first + tiles * P, :].rearrange("(g p) n -> p g n", p=P),
+                    in_=result[:, g : g + tiles, :],
+                )
 
+        last = BLOCKS - 1
         e1_of, planes_of, quantised_of, product_of = {}, {}, {}, {}
         scaled_of, output_of, turned_of = {}, {}, {}
-        for r in range(BLOCKS + 4):
-            operand = operand_of[min(r, BLOCKS - 1) // BLOCKS_PER_GRAPH]
+        for r in range(BLOCKS):
+            operand = operand_of[r // BLOCKS_PER_GRAPH]
+            e1_of[r] = hidden.tile([P, PASSES, PAIRS, PACK], BF16, align_bytes=64, name="e1")
             for ft in range(FEATURE_TILES):
                 c, t = divmod(ft, PACK)
-                if r < BLOCKS:
-                    if ft == 0:
-                        e1_of[r] = hidden.tile([P, PASSES, PAIRS, PACK], BF16, align_bytes=64, name="e1")
-                    if t == 0:
-                        planes_of[r, c] = planes.tile([P, PACK, PAIRS], BF16, name="e1_planes")
-                    first_layer(r, ft, operand, planes_of[r, c][:, t, :])
-                    if t == PACK - 1:
-                        regroup(planes_of[r, c], e1_of[r], c)
-                if ft == 0 and 3 <= r < BLOCKS + 3:
+                if t == 0:
+                    planes_of[r, c] = planes.tile([P, PACK, PAIRS], BF16, name="e1_planes")
+                first_layer(r, ft, operand, planes_of[r, c][:, t, :])
+                if t == PACK - 1 and (r, c) != (last, PASSES - 1):
+                    regroup(planes_of[r, c], e1_of[r], c)
+                if ft == 0 and 3 <= r:
                     scaled_of[r - 3] = scale_product(product_of[r - 3])
                 if ft == 0 and 4 <= r:
                     turned_of[r - 4] = turn(output_of[r - 4])
-                if ft == 3 and 1 <= r <= BLOCKS:
+                if ft == 3 and 1 <= r:
                     regroup_rest(planes_of[r - 1, 1], e1_of[r - 1], 1)
-                if ft == 3 and 3 <= r < BLOCKS + 3:
+                if ft == 3 and 3 <= r:
                     output_of[r - 3] = second_leaky_relu(*scaled_of[r - 3])
                 if ft == 3 and 4 <= r:
                     store(r - 4, turned_of[r - 4])
-                if ft == 4 and 2 <= r < BLOCKS + 2:
+                if ft == 4 and 2 <= r:
                     product_of[r - 2] = second_product(*quantised_of[r - 2])
-                if ft == 7 and r < BLOCKS:
+                if ft == 7:
                     regroup_rest(planes_of[r, 0], e1_of[r], 0)
-                if ft == 7 and 1 <= r <= BLOCKS:
-                    quantised_of[r - 1] = quantise(e1_of[r - 1])
+                if ft == 7 and 1 <= r:
+                    quantised_of[r - 1] = quantised_tiles()
+                    quantise(e1_of[r - 1], quantised_of[r - 1], slice(0, PASSES))
                 if r == 0 and ft == 3:
                     fill_rows(0, operand, I_PER_BLOCK, NODES)
                 if r == 0 and ft == 4:
@@ -379,3 +402,22 @@ def tile_graph_gan_pa_t_kernel(tc, x, fe_w0, fe_b0, fe_w1, fe_b1, out):
                 next_graph = (r + 2) // BLOCKS_PER_GRAPH
                 operand_of[next_graph] = pair_operands(next_graph)
                 fill_rows(next_graph, operand_of[next_graph], 0, NODES)
+
+        quantised_of[last] = quantised_tiles()
+        quantise(e1_of[last], quantised_of[last], slice(0, 1))
+        regroup_last(planes_of[last, 1], e1_of[last], 1)
+        quantise(e1_of[last], quantised_of[last], slice(1, PASSES))
+        turned_of[last - 3] = turn(output_of[last - 3])
+        scaled_of[last - 2] = scale_product(product_of[last - 2])
+        product_of[last - 1] = second_product(*quantised_of[last - 1], psum_z, "z")
+        product_of[last] = second_product(*quantised_of[last], psum_z, "z")
+        store(last - 3, turned_of[last - 3])
+        scaled_of[last - 1] = scale_product(product_of[last - 1])
+        scaled_of[last] = scale_product(product_of[last], pieces=2)
+        for block in (last - 2, last - 1, last):
+            output_of[block] = second_leaky_relu(*scaled_of[block])
+        for block in (last - 2, last - 1, last):
+            turned_of[block] = turn(output_of[block], psum_z, "z")
+        for block in (last - 2, last - 1):
+            store(block, turned_of[block])
+        store(last, turned_of[last], pieces=2)

@@ -26,14 +26,15 @@ PASSES = HIDDEN // K_PASS
 FEATURE_TILES = HIDDEN // P
 ALPHA = 0.2
 
-I_PER_BLOCK = 8
-PAIRS = I_PER_BLOCK * NODES
+SIDE = 16
+SQUARE = SIDE * SIDE
+SQUARES_PER_BLOCK = 2
+PAIRS = SQUARES_PER_BLOCK * SQUARE
 PAIR_TILES = PAIRS // P
-BLOCKS = ROWS // I_PER_BLOCK
-BLOCKS_PER_GRAPH = NODES // I_PER_BLOCK
-J_HALF = 32
-HALF_PAIRS = I_PER_BLOCK * J_HALF
-J_HALVES = NODES // J_HALF
+BLOCKS_PER_BAND = 2
+SIDES = NODES // SIDE
+BLOCKS = ROWS * NODES // PAIRS
+BLOCKS_PER_GRAPH = NODES * NODES // PAIRS
 SCALAR_WORDS = 64
 LAST_SCALAR_WORDS = 288
 
@@ -57,7 +58,7 @@ def tile_graph_gan_pa_t_kernel(tc, x, fe_w0, fe_b0, fe_w1, fe_b1, out):
         lines = stack.enter_context(tc.tile_pool(name="lines", bufs=8))
         planes = stack.enter_context(tc.tile_pool(name="planes", bufs=4))
         hidden = stack.enter_context(tc.tile_pool(name="hidden", bufs=3))
-        results = stack.enter_context(tc.tile_pool(name="results", bufs=3))
+        results = stack.enter_context(tc.tile_pool(name="results", bufs=5))
         operands = stack.enter_context(tc.tile_pool(name="operands", bufs=2))
         psum_z = stack.enter_context(tc.psum_pool(name="psum_z", bufs=5))
         psum_out = stack.enter_context(tc.psum_pool(name="psum_out", bufs=2))
@@ -128,48 +129,52 @@ def tile_graph_gan_pa_t_kernel(tc, x, fe_w0, fe_b0, fe_w1, fe_b1, out):
 
         def pair_operands(graph):
             rows = slice(graph * NODES, (graph + 1) * NODES)
-            codes_i = operands.tile([P, NODES, J_HALF], U32, align_bytes=64)
-            scales_i = operands.tile([P, NODES, J_HALF], U8, align_bytes=64)
-            codes_j = operands.tile([P, J_HALVES, I_PER_BLOCK, J_HALF], U32, align_bytes=64)
-            scales_j = operands.tile([P, J_HALVES, I_PER_BLOCK, J_HALF], U8, align_bytes=64)
-            codes = x_codes[:, rows].bitcast(I32)
-            words = x_scales[:, rows].bitcast(I32)
-            for half in range(J_HALVES):
-                nc.vector.tensor_copy(
-                    out=codes_j[:, half, :, :].bitcast(I32),
-                    in_=codes[:, half * J_HALF : (half + 1) * J_HALF]
-                    .unsqueeze(1)
-                    .to_broadcast([P, I_PER_BLOCK, J_HALF]),
-                )
-                nc.vector.tensor_copy(
-                    out=scales_j[:, half, :, :]
-                    .rearrange("p i j -> p (i j)")
-                    .bitcast(I32)
-                    .rearrange("p (i w) -> p i w", i=I_PER_BLOCK),
-                    in_=words[:, half * J_HALF // 4 : (half + 1) * J_HALF // 4]
-                    .unsqueeze(1)
-                    .to_broadcast([P, I_PER_BLOCK, J_HALF // 4]),
-                )
+            codes_i = operands.tile([P, NODES, SIDE], U32, align_bytes=64)
+            scales_i = operands.tile([P, NODES, SIDE], U8, align_bytes=64)
+            codes_j = operands.tile([P, SIDES, SIDE, SIDE], U32, align_bytes=64)
+            scales_j = operands.tile([P, SIDES, SIDE, SIDE], U8, align_bytes=64)
+            nc.vector.tensor_copy(
+                out=codes_j[:].bitcast(I32),
+                in_=x_codes[:, rows]
+                .bitcast(I32)
+                .rearrange("p (q j) -> p q j", q=SIDES)
+                .unsqueeze(2)
+                .to_broadcast([P, SIDES, SIDE, SIDE]),
+            )
+            nc.vector.tensor_copy(
+                out=scales_j[:]
+                .rearrange("p q i j -> p (q i j)")
+                .bitcast(I32)
+                .rearrange("p (q i w) -> p q i w", q=SIDES, i=SIDE),
+                in_=x_scales[:, rows]
+                .bitcast(I32)
+                .rearrange("p (q w) -> p q w", q=SIDES)
+                .unsqueeze(2)
+                .to_broadcast([P, SIDES, SIDE, SIDE // 4]),
+            )
             return codes_i, scales_i, codes_j, scales_j
+
+        bytes_4 = keep.tile([P, ROWS, 4], U8, align_bytes=64)
+
+        def widen_scales(first, last):
+            for n in range(4):
+                nc.vector.tensor_copy(out=bytes_4[:, first:last, n], in_=x_scales[:, first:last])
 
         def fill_rows(graph, operand, first, last):
             codes_i, scales_i = operand[:2]
             count = last - first
             rows = slice(graph * NODES + first, graph * NODES + last)
-            bytes_4 = operands.tile([P, NODES, 4], U8, align_bytes=64)
-            for n in range(4):
-                nc.vector.tensor_copy(out=bytes_4[:, :count, n], in_=x_scales[:, rows])
             nc.vector.tensor_copy(
                 out=codes_i[:, first:last, :].bitcast(I32),
-                in_=x_codes[:, rows].bitcast(I32).unsqueeze(2).to_broadcast([P, count, J_HALF]),
+                in_=x_codes[:, rows].bitcast(I32).unsqueeze(2).to_broadcast([P, count, SIDE]),
             )
-            words_4 = bytes_4[:].rearrange("p i n -> p (i n)").bitcast(I32)
+            words_4 = bytes_4[:, rows, :].rearrange("p i n -> p (i n)").bitcast(I32)
             nc.vector.tensor_copy(
                 out=scales_i[:, first:last, :]
                 .rearrange("p i j -> p (i j)")
                 .bitcast(I32)
                 .rearrange("p (i w) -> p i w", i=count),
-                in_=words_4[:, :count].unsqueeze(2).to_broadcast([P, count, J_HALF // 4]),
+                in_=words_4.unsqueeze(2).to_broadcast([P, count, SIDE // 4]),
             )
 
         biases = keep.tile([P, FEATURE_TILES], F32)
@@ -209,7 +214,8 @@ def tile_graph_gan_pa_t_kernel(tc, x, fe_w0, fe_b0, fe_w1, fe_b1, out):
         group_w0(nc.scalar.copy, 0, 1)
         quantise_x(0)
         operand_of = {0: pair_operands(0)}
-        fill_rows(0, operand_of[0], 0, I_PER_BLOCK)
+        widen_scales(0, SIDE)
+        fill_rows(0, operand_of[0], 0, SIDE)
         quantise_w0(0, 0)
         quantise_w0(0, 1)
         group_w0(nc.vector.tensor_copy, 1, 0)
@@ -235,14 +241,15 @@ def tile_graph_gan_pa_t_kernel(tc, x, fe_w0, fe_b0, fe_w1, fe_b1, out):
 
         def first_layer(block, ft, operand, plane):
             codes_i, scales_i, codes_j, scales_j = operand
-            i_first = block % BLOCKS_PER_GRAPH * I_PER_BLOCK
-            i_rows = slice(i_first, i_first + I_PER_BLOCK)
+            band, half = divmod(block % BLOCKS_PER_GRAPH, BLOCKS_PER_BAND)
+            i_rows = slice(band * SIDE, (band + 1) * SIDE)
             tile_cols = slice(ft * P, (ft + 1) * P)
             bank = psum_z.tile([P, PAIRS], F32, tag="z")
-            for half in range(J_HALVES):
-                half_bank = bank[:, half * HALF_PAIRS : (half + 1) * HALF_PAIRS]
+            for s in range(SQUARES_PER_BLOCK):
+                square = bank[:, s * SQUARE : (s + 1) * SQUARE]
+                q = half * SQUARES_PER_BLOCK + s
                 nc.tensor.matmul_mx(
-                    out=half_bank,
+                    out=square,
                     lhsT=w0_codes[:, 0, tile_cols].bitcast(FP8X4),
                     lhsT_scale=w0_scales[:, 0, tile_cols],
                     rhs=codes_i[:, i_rows, :].rearrange("p i j -> p (i j)").bitcast(FP8X4),
@@ -251,11 +258,11 @@ def tile_graph_gan_pa_t_kernel(tc, x, fe_w0, fe_b0, fe_w1, fe_b1, out):
                     stop=False,
                 )
                 nc.tensor.matmul_mx(
-                    out=half_bank,
+                    out=square,
                     lhsT=w0_codes[:, 1, tile_cols].bitcast(FP8X4),
                     lhsT_scale=w0_scales[:, 1, tile_cols],
-                    rhs=codes_j[:, half, :, :].rearrange("p i j -> p (i j)").bitcast(FP8X4),
-                    rhs_scale=scales_j[:, half, :, :].rearrange("p i j -> p (i j)"),
+                    rhs=codes_j[:, q, :, :].rearrange("p i j -> p (i j)").bitcast(FP8X4),
+                    rhs_scale=scales_j[:, q, :, :].rearrange("p i j -> p (i j)"),
                     start=False,
                     stop=True,
                 )
@@ -316,9 +323,9 @@ def tile_graph_gan_pa_t_kernel(tc, x, fe_w0, fe_b0, fe_w1, fe_b1, out):
                 )
             return y_t
 
-        def scale_product(y_t, pieces=1):
+        def scale_product(y_t, parts=1):
             scaled = results.tile([P, PAIRS], F32)
-            width = PAIRS // pieces
+            width = PAIRS // parts
             for first in range(0, PAIRS, width):
                 columns = slice(first, first + width)
                 nc.scalar.activation(
@@ -326,37 +333,43 @@ def tile_graph_gan_pa_t_kernel(tc, x, fe_w0, fe_b0, fe_w1, fe_b1, out):
                 )
             return y_t, scaled
 
-        def second_leaky_relu(y_t, scaled):
-            out_t = results.tile([P, PAIRS], F32)
-            ordered = out_t[:].rearrange("p (i h j) -> p h i j", i=I_PER_BLOCK, h=J_HALVES)
-            for half in range(J_HALVES):
-                cols = slice(half * HALF_PAIRS, (half + 1) * HALF_PAIRS)
+        output_of = {}
+
+        def second_leaky_relu(block, y_t, scaled):
+            band, half = divmod(block, BLOCKS_PER_BAND)
+            if half == 0:
+                output_of[band] = results.tile([P, SIDE * NODES], F32, name="out_t")
+            ordered = output_of[band][:].rearrange("p (i q j) -> p q i j", i=SIDE, q=SIDES)
+            for s in range(SQUARES_PER_BLOCK):
+                cols = slice(s * SQUARE, (s + 1) * SQUARE)
                 nc.vector.scalar_tensor_tensor(
-                    out=ordered[:, half, :, :],
-                    in0=y_t[:, cols].rearrange("p (i j) -> p i j", i=I_PER_BLOCK),
+                    out=ordered[:, half * SQUARES_PER_BLOCK + s, :, :],
+                    in0=y_t[:, cols].rearrange("p (i j) -> p i j", i=SIDE),
                     scalar=b1,
-                    in1=scaled[:, cols].rearrange("p (i j) -> p i j", i=I_PER_BLOCK),
+                    in1=scaled[:, cols].rearrange("p (i j) -> p i j", i=SIDE),
                     op0=ADD,
                     op1=MAX,
                 )
-            return out_t
 
-        def turn(out_t, pool=psum_turn, tag="turned"):
+        def turn(piece, pool=psum_turn, tag="turned"):
+            band, half = divmod(piece, BLOCKS_PER_BAND)
             turned = pool.tile([P, PAIRS], F32, tag=tag)
             for g in range(PAIR_TILES):
-                columns = slice(g * P, (g + 1) * P)
-                nc.tensor.transpose(turned[:, columns], out_t[:, columns], identity_f32[:])
+                first = half * PAIRS + g * P
+                nc.tensor.transpose(
+                    turned[:, g * P : (g + 1) * P], output_of[band][:, first : first + P], identity_f32[:]
+                )
             return turned
 
-        def store(block, turned, pieces=1):
+        def store(piece, turned, parts=1, copy=nc.scalar.copy):
             result = results.tile([P, PAIR_TILES, D_OUT], F32)
-            tiles = PAIR_TILES // pieces
+            tiles = PAIR_TILES // parts
             for g in range(0, PAIR_TILES, tiles):
-                nc.scalar.copy(
+                copy(
                     out=result[:, g : g + tiles, :].rearrange("p g n -> p (g n)"),
                     in_=turned[:, g * P : (g + tiles) * P],
                 )
-                first = block * PAIRS + g * P
+                first = piece * PAIRS + g * P
                 nc.sync.dma_start(
                     out=out_rows[first : first + tiles * P, :].rearrange("(g p) n -> p g n", p=P),
                     in_=result[:, g : g + tiles, :],
@@ -364,7 +377,7 @@ def tile_graph_gan_pa_t_kernel(tc, x, fe_w0, fe_b0, fe_w1, fe_b1, out):
 
         last = BLOCKS - 1
         e1_of, planes_of, quantised_of, product_of = {}, {}, {}, {}
-        scaled_of, output_of, turned_of = {}, {}, {}
+        scaled_of, turned_of = {}, {}
         for r in range(BLOCKS):
             operand = operand_of[r // BLOCKS_PER_GRAPH]
             e1_of[r] = hidden.tile([P, PASSES, PAIRS, PACK], BF16, align_bytes=64, name="e1")
@@ -377,14 +390,14 @@ def tile_graph_gan_pa_t_kernel(tc, x, fe_w0, fe_b0, fe_w1, fe_b1, out):
                     regroup(planes_of[r, c], e1_of[r], c)
                 if ft == 0 and 3 <= r:
                     scaled_of[r - 3] = scale_product(product_of[r - 3])
-                if ft == 0 and 4 <= r:
-                    turned_of[r - 4] = turn(output_of[r - 4])
+                if ft == 0 and 5 <= r:
+                    turned_of[r - 5] = turn(r - 5)
                 if ft == 3 and 1 <= r:
                     regroup_rest(planes_of[r - 1, 1], e1_of[r - 1], 1)
                 if ft == 3 and 3 <= r:
-                    output_of[r - 3] = second_leaky_relu(*scaled_of[r - 3])
-                if ft == 3 and 4 <= r:
-                    store(r - 4, turned_of[r - 4])
+                    second_leaky_relu(r - 3, *scaled_of[r - 3])
+                if ft == 3 and 5 <= r:
+                    store(r - 5, turned_of[r - 5])
                 if ft == 4 and 2 <= r:
                     product_of[r - 2] = second_product(*quantised_of[r - 2])
                 if ft == 7:
@@ -393,10 +406,12 @@ def tile_graph_gan_pa_t_kernel(tc, x, fe_w0, fe_b0, fe_w1, fe_b1, out):
                     quantised_of[r - 1] = quantised_tiles()
                     quantise(e1_of[r - 1], quantised_of[r - 1], slice(0, PASSES))
                 if r == 0 and ft == 3:
-                    fill_rows(0, operand, I_PER_BLOCK, NODES)
+                    widen_scales(SIDE, NODES)
+                    fill_rows(0, operand, SIDE, NODES)
                 if r == 0 and ft == 4:
                     group_w1()
                 if r == 0 and ft == 7:
+                    widen_scales(NODES, ROWS)
                     quantise_w1()
             if r + 2 < BLOCKS and (r + 2) % BLOCKS_PER_GRAPH == 0:
                 next_graph = (r + 2) // BLOCKS_PER_GRAPH
@@ -407,17 +422,18 @@ def tile_graph_gan_pa_t_kernel(tc, x, fe_w0, fe_b0, fe_w1, fe_b1, out):
         quantise(e1_of[last], quantised_of[last], slice(0, 1))
         regroup_last(planes_of[last, 1], e1_of[last], 1)
         quantise(e1_of[last], quantised_of[last], slice(1, PASSES))
-        turned_of[last - 3] = turn(output_of[last - 3])
+        turned_of[last - 4] = turn(last - 4)
         scaled_of[last - 2] = scale_product(product_of[last - 2])
         product_of[last - 1] = second_product(*quantised_of[last - 1], psum_z, "z")
         product_of[last] = second_product(*quantised_of[last], psum_z, "z")
-        store(last - 3, turned_of[last - 3])
+        store(last - 4, turned_of[last - 4])
         scaled_of[last - 1] = scale_product(product_of[last - 1])
-        scaled_of[last] = scale_product(product_of[last], pieces=2)
+        scaled_of[last] = scale_product(product_of[last], parts=2)
         for block in (last - 2, last - 1, last):
-            output_of[block] = second_leaky_relu(*scaled_of[block])
-        for block in (last - 2, last - 1, last):
-            turned_of[block] = turn(output_of[block], psum_z, "z")
-        for block in (last - 2, last - 1):
-            store(block, turned_of[block])
-        store(last, turned_of[last], pieces=2)
+            second_leaky_relu(block, *scaled_of[block])
+        for piece in (last - 3, last - 2, last - 1, last):
+            turned_of[piece] = turn(piece, psum_z, "z")
+        for piece in (last - 3, last - 2):
+            store(piece, turned_of[piece])
+        store(last - 1, turned_of[last - 1], copy=nc.vector.tensor_copy)
+        store(last, turned_of[last], parts=2)

@@ -13,6 +13,7 @@ ADD = mybir.AluOpType.add
 MULT = mybir.AluOpType.mult
 MAX = mybir.AluOpType.max
 IDENTITY = mybir.ActivationFunctionType.Identity
+RELU = mybir.ActivationFunctionType.Relu
 
 P = 128
 PACK = 4
@@ -35,8 +36,10 @@ BLOCKS_PER_BAND = 2
 SIDES = NODES // SIDE
 BLOCKS = ROWS * NODES // PAIRS
 BLOCKS_PER_GRAPH = NODES * NODES // PAIRS
-SCALAR_WORDS = 64
+SCALAR_WORDS = 32
 LAST_SCALAR_WORDS = 288
+VECTOR_NODES = 8
+SCALAR_NODES = SIDE - VECTOR_NODES
 
 FLOPS = 2 * HALVES * ROWS * D_IN * HIDDEN + 2 * ROWS * NODES * HIDDEN * D_OUT
 
@@ -188,6 +191,8 @@ def tile_graph_gan_pa_t_kernel(tc, x, fe_w0, fe_b0, fe_w1, fe_b1, out):
         b1 = b1_tile[:]
         b1_scaled = keep.tile([P, 1], F32)
         nc.gpsimd.tensor_scalar(out=b1_scaled[:], in0=b1, scalar1=ALPHA, scalar2=0.0, op0=MULT, op1=ADD)
+        b1_rest = keep.tile([P, 1], F32)
+        nc.gpsimd.tensor_scalar(out=b1_rest[:], in0=b1, scalar1=1.0 - ALPHA, scalar2=0.0, op0=MULT, op1=ADD)
 
         w0_grouped = keep.tile([P, HALVES, HIDDEN, PACK], BF16, align_bytes=64)
         w0_codes = keep.tile([P, HALVES, HIDDEN], U32, align_bytes=64)
@@ -277,8 +282,8 @@ def tile_graph_gan_pa_t_kernel(tc, x, fe_w0, fe_b0, fe_w1, fe_b1, out):
         def regroup(e1_planes, e1, c):
             cut = PAIRS - SCALAR_WORDS
             nc.gpsimd.tensor_scalar(
-                out=e1[:, c, :cut, :],
-                in0=e1_planes[:, :, :cut].rearrange("p t w -> p w t"),
+                out=e1[:, c, :cut, :].rearrange("p (g i) t -> p g t i", i=4),
+                in0=e1_planes[:, :, :cut].rearrange("p t (g i) -> p g t i", i=4),
                 scalar1=1.0,
                 scalar2=0.0,
                 op0=MULT,
@@ -323,13 +328,36 @@ def tile_graph_gan_pa_t_kernel(tc, x, fe_w0, fe_b0, fe_w1, fe_b1, out):
                 )
             return y_t
 
-        def scale_product(y_t, parts=1):
-            scaled = results.tile([P, PAIRS], F32)
-            width = PAIRS // parts
-            for first in range(0, PAIRS, width):
-                columns = slice(first, first + width)
+        parts_of = {}
+
+        def scale_product(block, y_t):
+            band, half = divmod(block, BLOCKS_PER_BAND)
+            squares = y_t[:].rearrange("p (s i j) -> p s i j", s=SQUARES_PER_BLOCK, i=SIDE)
+            scaled = results.tile([P, SQUARES_PER_BLOCK, VECTOR_NODES, SIDE], F32)
+            nc.scalar.activation(
+                out=scaled[:],
+                in_=squares[:, :, :VECTOR_NODES, :],
+                func=IDENTITY,
+                bias=b1_scaled[:],
+                scale=ALPHA,
+            )
+            if half == 0:
+                parts_of[band] = (
+                    results.tile([P, SCALAR_NODES * NODES], F32, name="linear"),
+                    results.tile([P, SCALAR_NODES * NODES], F32, name="positive"),
+                )
+            q = half * SQUARES_PER_BLOCK
+            for part, func, bias, scale in (
+                (parts_of[band][0], IDENTITY, b1_scaled, ALPHA),
+                (parts_of[band][1], RELU, b1_rest, 1.0 - ALPHA),
+            ):
+                ordered = part[:].rearrange("p (i q j) -> p q i j", i=SCALAR_NODES, q=SIDES)
                 nc.scalar.activation(
-                    out=scaled[:, columns], in_=y_t[:, columns], func=IDENTITY, bias=b1_scaled[:], scale=ALPHA
+                    out=ordered[:, q : q + SQUARES_PER_BLOCK, :, :],
+                    in_=squares[:, :, VECTOR_NODES:, :],
+                    func=func,
+                    bias=bias[:],
+                    scale=scale,
                 )
             return y_t, scaled
 
@@ -338,15 +366,15 @@ def tile_graph_gan_pa_t_kernel(tc, x, fe_w0, fe_b0, fe_w1, fe_b1, out):
         def second_leaky_relu(block, y_t, scaled):
             band, half = divmod(block, BLOCKS_PER_BAND)
             if half == 0:
-                output_of[band] = results.tile([P, SIDE * NODES], F32, name="out_t")
-            ordered = output_of[band][:].rearrange("p (i q j) -> p q i j", i=SIDE, q=SIDES)
+                output_of[band] = results.tile([P, VECTOR_NODES * NODES], F32, name="out_t")
+            ordered = output_of[band][:].rearrange("p (i q j) -> p q i j", i=VECTOR_NODES, q=SIDES)
+            squares = y_t[:].rearrange("p (s i j) -> p s i j", s=SQUARES_PER_BLOCK, i=SIDE)
             for s in range(SQUARES_PER_BLOCK):
-                cols = slice(s * SQUARE, (s + 1) * SQUARE)
                 nc.vector.scalar_tensor_tensor(
                     out=ordered[:, half * SQUARES_PER_BLOCK + s, :, :],
-                    in0=y_t[:, cols].rearrange("p (i j) -> p i j", i=SIDE),
+                    in0=squares[:, s, :VECTOR_NODES, :],
                     scalar=b1,
-                    in1=scaled[:, cols].rearrange("p (i j) -> p i j", i=SIDE),
+                    in1=scaled[:, s, :, :],
                     op0=ADD,
                     op1=MAX,
                 )
@@ -354,11 +382,17 @@ def tile_graph_gan_pa_t_kernel(tc, x, fe_w0, fe_b0, fe_w1, fe_b1, out):
         def turn(piece, pool=psum_turn, tag="turned"):
             band, half = divmod(piece, BLOCKS_PER_BAND)
             turned = pool.tile([P, PAIRS], F32, tag=tag)
+            sources = (output_of[band],) if half == 0 else parts_of[band]
             for g in range(PAIR_TILES):
-                first = half * PAIRS + g * P
-                nc.tensor.transpose(
-                    turned[:, g * P : (g + 1) * P], output_of[band][:, first : first + P], identity_f32[:]
-                )
+                for n, source in enumerate(sources):
+                    nc.tensor.matmul(
+                        turned[:, g * P : (g + 1) * P],
+                        lhsT=source[:, g * P : (g + 1) * P],
+                        rhs=identity_f32[:],
+                        is_transpose=True,
+                        start=(n == 0),
+                        stop=(n == len(sources) - 1),
+                    )
             return turned
 
         def store(piece, turned, parts=1, copy=nc.scalar.copy):
@@ -389,7 +423,7 @@ def tile_graph_gan_pa_t_kernel(tc, x, fe_w0, fe_b0, fe_w1, fe_b1, out):
                 if t == PACK - 1 and (r, c) != (last, PASSES - 1):
                     regroup(planes_of[r, c], e1_of[r], c)
                 if ft == 0 and 3 <= r:
-                    scaled_of[r - 3] = scale_product(product_of[r - 3])
+                    scaled_of[r - 3] = scale_product(r - 3, product_of[r - 3])
                 if ft == 0 and 5 <= r:
                     turned_of[r - 5] = turn(r - 5)
                 if ft == 3 and 1 <= r:
@@ -423,12 +457,12 @@ def tile_graph_gan_pa_t_kernel(tc, x, fe_w0, fe_b0, fe_w1, fe_b1, out):
         regroup_last(planes_of[last, 1], e1_of[last], 1)
         quantise(e1_of[last], quantised_of[last], slice(1, PASSES))
         turned_of[last - 4] = turn(last - 4)
-        scaled_of[last - 2] = scale_product(product_of[last - 2])
+        scaled_of[last - 2] = scale_product(last - 2, product_of[last - 2])
         product_of[last - 1] = second_product(*quantised_of[last - 1], psum_z, "z")
         product_of[last] = second_product(*quantised_of[last], psum_z, "z")
         store(last - 4, turned_of[last - 4])
-        scaled_of[last - 1] = scale_product(product_of[last - 1])
-        scaled_of[last] = scale_product(product_of[last], parts=2)
+        scaled_of[last - 1] = scale_product(last - 1, product_of[last - 1])
+        scaled_of[last] = scale_product(last, product_of[last])
         for block in (last - 2, last - 1, last):
             second_leaky_relu(block, *scaled_of[block])
         for piece in (last - 3, last - 2, last - 1, last):

@@ -36,7 +36,6 @@ BLOCKS_PER_BAND = 2
 SIDES = NODES // SIDE
 BLOCKS = ROWS * NODES // PAIRS
 BLOCKS_PER_GRAPH = NODES * NODES // PAIRS
-SCALAR_WORDS = 32
 LAST_SCALAR_WORDS = 288
 VECTOR_NODES = 8
 SCALAR_NODES = SIDE - VECTOR_NODES
@@ -280,19 +279,14 @@ def tile_graph_gan_pa_t_kernel(tc, x, fe_w0, fe_b0, fe_w1, fe_b1, out):
             )
 
         def regroup(e1_planes, e1, c):
-            cut = PAIRS - SCALAR_WORDS
             nc.gpsimd.tensor_scalar(
-                out=e1[:, c, :cut, :].rearrange("p (g i) t -> p g t i", i=4),
-                in0=e1_planes[:, :, :cut].rearrange("p t (g i) -> p g t i", i=4),
+                out=e1[:, c, :, :].rearrange("p (g i) t -> p g t i", i=4),
+                in0=e1_planes[:].rearrange("p t (g i) -> p g t i", i=4),
                 scalar1=1.0,
                 scalar2=0.0,
                 op0=MULT,
                 op1=ADD,
             )
-
-        def regroup_rest(e1_planes, e1, c):
-            cut = PAIRS - SCALAR_WORDS
-            side_by_side(nc.scalar.copy, e1[:, c, cut:, :], e1_planes[:, :, cut:])
 
         def regroup_last(e1_planes, e1, c):
             cut = PAIRS - LAST_SCALAR_WORDS
@@ -426,16 +420,12 @@ def tile_graph_gan_pa_t_kernel(tc, x, fe_w0, fe_b0, fe_w1, fe_b1, out):
                     scaled_of[r - 3] = scale_product(r - 3, product_of[r - 3])
                 if ft == 0 and 5 <= r:
                     turned_of[r - 5] = turn(r - 5)
-                if ft == 3 and 1 <= r:
-                    regroup_rest(planes_of[r - 1, 1], e1_of[r - 1], 1)
                 if ft == 3 and 3 <= r:
                     second_leaky_relu(r - 3, *scaled_of[r - 3])
                 if ft == 3 and 5 <= r:
                     store(r - 5, turned_of[r - 5])
                 if ft == 4 and 2 <= r:
                     product_of[r - 2] = second_product(*quantised_of[r - 2])
-                if ft == 7:
-                    regroup_rest(planes_of[r, 0], e1_of[r], 0)
                 if ft == 7 and 1 <= r:
                     quantised_of[r - 1] = quantised_tiles()
                     quantise(e1_of[r - 1], quantised_of[r - 1], slice(0, PASSES))

@@ -376,12 +376,14 @@ def tile_graph_gan_pa_t_kernel(tc, x, fe_w0, fe_b0, fe_w1, fe_b1, out):
         def turn(piece, pool=psum_turn, tag="turned"):
             band, half = divmod(piece, BLOCKS_PER_BAND)
             turned = pool.tile([P, PAIRS], F32, tag=tag)
-            sources = (output_of[band],) if half == 0 else parts_of[band]
             for g in range(PAIR_TILES):
+                first = (half * PAIR_TILES + g) * P
+                sources = (output_of[band],) if first < VECTOR_NODES * NODES else parts_of[band]
+                first -= 0 if len(sources) == 1 else VECTOR_NODES * NODES
                 for n, source in enumerate(sources):
                     nc.tensor.matmul(
                         turned[:, g * P : (g + 1) * P],
-                        lhsT=source[:, g * P : (g + 1) * P],
+                        lhsT=source[:, first : first + P],
                         rhs=identity_f32[:],
                         is_transpose=True,
                         start=(n == 0),
@@ -406,38 +408,43 @@ def tile_graph_gan_pa_t_kernel(tc, x, fe_w0, fe_b0, fe_w1, fe_b1, out):
         last = BLOCKS - 1
         e1_of, planes_of, quantised_of, product_of = {}, {}, {}, {}
         scaled_of, turned_of = {}, {}
+        order = [(0, 0)]
         for r in range(BLOCKS):
+            order.extend((r, ft) for ft in range(1, FEATURE_TILES - 1))
+            order.extend([(r + 1, 0)] if r < last else [])
+            order.append((r, FEATURE_TILES - 1))
+        for r, ft in order:
             operand = operand_of[r // BLOCKS_PER_GRAPH]
-            e1_of[r] = hidden.tile([P, PASSES, PAIRS, PACK], BF16, align_bytes=64, name="e1")
-            for ft in range(FEATURE_TILES):
-                c, t = divmod(ft, PACK)
-                if t == 0:
-                    planes_of[r, c] = planes.tile([P, PACK, PAIRS], BF16, name="e1_planes")
-                first_layer(r, ft, operand, planes_of[r, c][:, t, :])
-                if t == PACK - 1 and (r, c) != (last, PASSES - 1):
-                    regroup(planes_of[r, c], e1_of[r], c)
-                if ft == 0 and 3 <= r:
-                    scaled_of[r - 3] = scale_product(r - 3, product_of[r - 3])
-                if ft == 0 and 5 <= r:
-                    turned_of[r - 5] = turn(r - 5)
-                if ft == 3 and 3 <= r:
-                    second_leaky_relu(r - 3, *scaled_of[r - 3])
-                if ft == 3 and 5 <= r:
-                    store(r - 5, turned_of[r - 5])
-                if ft == 4 and 2 <= r:
-                    product_of[r - 2] = second_product(*quantised_of[r - 2])
-                if ft == 7 and 1 <= r:
-                    quantised_of[r - 1] = quantised_tiles()
-                    quantise(e1_of[r - 1], quantised_of[r - 1], slice(0, PASSES))
-                if r == 0 and ft == 3:
-                    widen_scales(SIDE, NODES)
-                    fill_rows(0, operand, SIDE, NODES)
-                if r == 0 and ft == 4:
-                    group_w1()
-                if r == 0 and ft == 7:
-                    widen_scales(NODES, ROWS)
-                    quantise_w1()
-            if r + 2 < BLOCKS and (r + 2) % BLOCKS_PER_GRAPH == 0:
+            c, t = divmod(ft, PACK)
+            if ft == 0:
+                e1_of[r] = hidden.tile([P, PASSES, PAIRS, PACK], BF16, align_bytes=64, name="e1")
+            if t == 0:
+                planes_of[r, c] = planes.tile([P, PACK, PAIRS], BF16, name="e1_planes")
+            first_layer(r, ft, operand, planes_of[r, c][:, t, :])
+            if t == PACK - 1 and (r, c) != (last, PASSES - 1):
+                regroup(planes_of[r, c], e1_of[r], c)
+            if ft == 1 and 3 <= r:
+                scaled_of[r - 3] = scale_product(r - 3, product_of[r - 3])
+            if ft == 1 and 5 <= r:
+                turned_of[r - 5] = turn(r - 5)
+            if ft == 4 and 3 <= r:
+                second_leaky_relu(r - 3, *scaled_of[r - 3])
+            if ft == 4 and 5 <= r:
+                store(r - 5, turned_of[r - 5])
+            if ft == 5 and 2 <= r:
+                product_of[r - 2] = second_product(*quantised_of[r - 2])
+            if ft == 7 and 1 <= r:
+                quantised_of[r - 1] = quantised_tiles()
+                quantise(e1_of[r - 1], quantised_of[r - 1], slice(0, PASSES))
+            if r == 0 and ft == 0:
+                widen_scales(SIDE, NODES)
+                fill_rows(0, operand, SIDE, NODES)
+            if r == 0 and ft == 4:
+                group_w1()
+            if r == 0 and ft == 7:
+                quantise_w1()
+                widen_scales(NODES, ROWS)
+            if ft == 7 and r + 2 < BLOCKS and (r + 2) % BLOCKS_PER_GRAPH == 0:
                 next_graph = (r + 2) // BLOCKS_PER_GRAPH
                 operand_of[next_graph] = pair_operands(next_graph)
                 fill_rows(next_graph, operand_of[next_graph], 0, NODES)

@@ -135,14 +135,17 @@ def tile_graph_gan_pa_t_kernel(tc, x, fe_w0, fe_b0, fe_w1, fe_b1, out):
             scales_i = operands.tile([P, NODES, SIDE], U8, align_bytes=64)
             codes_j = operands.tile([P, SIDES, SIDE, SIDE], U32, align_bytes=64)
             scales_j = operands.tile([P, SIDES, SIDE, SIDE], U8, align_bytes=64)
-            nc.vector.tensor_copy(
-                out=codes_j[:].bitcast(I32),
-                in_=x_codes[:, rows]
-                .bitcast(I32)
-                .rearrange("p (q j) -> p q j", q=SIDES)
-                .unsqueeze(2)
-                .to_broadcast([P, SIDES, SIDE, SIDE]),
-            )
+            codes = x_codes[:, rows].bitcast(I32).rearrange("p (q j) -> p q j", q=SIDES)
+            if graph == 0:
+                nc.vector.tensor_copy(
+                    out=codes_j[:].bitcast(I32), in_=codes.unsqueeze(2).to_broadcast([P, SIDES, SIDE, SIDE])
+                )
+            else:
+                for q in range(SIDES):
+                    nc.sync.dma_start(
+                        out=codes_j[:, q, :, :].bitcast(I32),
+                        in_=codes[:, q, :].unsqueeze(1).to_broadcast([P, SIDE, SIDE]),
+                    )
             nc.vector.tensor_copy(
                 out=scales_j[:]
                 .rearrange("p q i j -> p (q i j)")
@@ -322,53 +325,45 @@ def tile_graph_gan_pa_t_kernel(tc, x, fe_w0, fe_b0, fe_w1, fe_b1, out):
                 )
             return y_t
 
-        parts_of = {}
+        linear_of, positive_of, maximum_of = {}, {}, {}
 
-        def scale_product(block, y_t):
+        def ordered(part, nodes):
+            return part[:].rearrange("p (i q j) -> p q i j", i=nodes, q=SIDES)
+
+        def second_parts(block, y_t):
             band, half = divmod(block, BLOCKS_PER_BAND)
+            if half == 0:
+                linear_of[band] = results.tile([P, SIDE * NODES], F32, name="linear")
+                positive_of[band] = results.tile([P, SCALAR_NODES * NODES], F32, name="positive")
+            runs = slice(half * SQUARES_PER_BLOCK, (half + 1) * SQUARES_PER_BLOCK)
             squares = y_t[:].rearrange("p (s i j) -> p s i j", s=SQUARES_PER_BLOCK, i=SIDE)
-            scaled = results.tile([P, SQUARES_PER_BLOCK, VECTOR_NODES, SIDE], F32)
             nc.scalar.activation(
-                out=scaled[:],
-                in_=squares[:, :, :VECTOR_NODES, :],
+                out=ordered(linear_of[band], SIDE)[:, runs, :, :],
+                in_=squares,
                 func=IDENTITY,
                 bias=b1_scaled[:],
                 scale=ALPHA,
             )
-            if half == 0:
-                parts_of[band] = (
-                    results.tile([P, SCALAR_NODES * NODES], F32, name="linear"),
-                    results.tile([P, SCALAR_NODES * NODES], F32, name="positive"),
-                )
-            q = half * SQUARES_PER_BLOCK
-            for part, func, bias, scale in (
-                (parts_of[band][0], IDENTITY, b1_scaled, ALPHA),
-                (parts_of[band][1], RELU, b1_rest, 1.0 - ALPHA),
-            ):
-                ordered = part[:].rearrange("p (i q j) -> p q i j", i=SCALAR_NODES, q=SIDES)
-                nc.scalar.activation(
-                    out=ordered[:, q : q + SQUARES_PER_BLOCK, :, :],
-                    in_=squares[:, :, VECTOR_NODES:, :],
-                    func=func,
-                    bias=bias[:],
-                    scale=scale,
-                )
-            return y_t, scaled
+            nc.scalar.activation(
+                out=ordered(positive_of[band], SCALAR_NODES)[:, runs, :, :],
+                in_=squares[:, :, VECTOR_NODES:, :],
+                func=RELU,
+                bias=b1_rest[:],
+                scale=1.0 - ALPHA,
+            )
 
-        output_of = {}
-
-        def second_leaky_relu(block, y_t, scaled):
+        def second_leaky_relu(block, y_t):
             band, half = divmod(block, BLOCKS_PER_BAND)
             if half == 0:
-                output_of[band] = results.tile([P, VECTOR_NODES * NODES], F32, name="out_t")
-            ordered = output_of[band][:].rearrange("p (i q j) -> p q i j", i=VECTOR_NODES, q=SIDES)
+                maximum_of[band] = results.tile([P, VECTOR_NODES * NODES], F32, name="maximum")
             squares = y_t[:].rearrange("p (s i j) -> p s i j", s=SQUARES_PER_BLOCK, i=SIDE)
             for s in range(SQUARES_PER_BLOCK):
+                q = half * SQUARES_PER_BLOCK + s
                 nc.vector.scalar_tensor_tensor(
-                    out=ordered[:, half * SQUARES_PER_BLOCK + s, :, :],
+                    out=ordered(maximum_of[band], VECTOR_NODES)[:, q, :, :],
                     in0=squares[:, s, :VECTOR_NODES, :],
                     scalar=b1,
-                    in1=scaled[:, s, :, :],
+                    in1=ordered(linear_of[band], SIDE)[:, q, :VECTOR_NODES, :],
                     op0=ADD,
                     op1=MAX,
                 )
@@ -378,16 +373,19 @@ def tile_graph_gan_pa_t_kernel(tc, x, fe_w0, fe_b0, fe_w1, fe_b1, out):
             turned = pool.tile([P, PAIRS], F32, tag=tag)
             for g in range(PAIR_TILES):
                 first = (half * PAIR_TILES + g) * P
-                sources = (output_of[band],) if first < VECTOR_NODES * NODES else parts_of[band]
-                first -= 0 if len(sources) == 1 else VECTOR_NODES * NODES
-                for n, source in enumerate(sources):
+                if first < VECTOR_NODES * NODES:
+                    columns = (maximum_of[band][:, first : first + P],)
+                else:
+                    rest = first - VECTOR_NODES * NODES
+                    columns = (linear_of[band][:, first : first + P], positive_of[band][:, rest : rest + P])
+                for n, part in enumerate(columns):
                     nc.tensor.matmul(
                         turned[:, g * P : (g + 1) * P],
-                        lhsT=source[:, first : first + P],
+                        lhsT=part,
                         rhs=identity_f32[:],
                         is_transpose=True,
                         start=(n == 0),
-                        stop=(n == len(sources) - 1),
+                        stop=(n == len(columns) - 1),
                     )
             return turned
 
@@ -407,7 +405,7 @@ def tile_graph_gan_pa_t_kernel(tc, x, fe_w0, fe_b0, fe_w1, fe_b1, out):
 
         last = BLOCKS - 1
         e1_of, planes_of, quantised_of, product_of = {}, {}, {}, {}
-        scaled_of, turned_of = {}, {}
+        turned_of = {}
         order = [(0, 0)]
         for r in range(BLOCKS):
             order.extend((r, ft) for ft in range(1, FEATURE_TILES - 1))
@@ -424,11 +422,11 @@ def tile_graph_gan_pa_t_kernel(tc, x, fe_w0, fe_b0, fe_w1, fe_b1, out):
             if t == PACK - 1 and (r, c) != (last, PASSES - 1):
                 regroup(planes_of[r, c], e1_of[r], c)
             if ft == 1 and 3 <= r:
-                scaled_of[r - 3] = scale_product(r - 3, product_of[r - 3])
+                second_parts(r - 3, product_of[r - 3])
             if ft == 1 and 5 <= r:
                 turned_of[r - 5] = turn(r - 5)
             if ft == 4 and 3 <= r:
-                second_leaky_relu(r - 3, *scaled_of[r - 3])
+                second_leaky_relu(r - 3, product_of[r - 3])
             if ft == 4 and 5 <= r:
                 store(r - 5, turned_of[r - 5])
             if ft == 5 and 2 <= r:
@@ -454,14 +452,14 @@ def tile_graph_gan_pa_t_kernel(tc, x, fe_w0, fe_b0, fe_w1, fe_b1, out):
         regroup_last(planes_of[last, 1], e1_of[last], 1)
         quantise(e1_of[last], quantised_of[last], slice(1, PASSES))
         turned_of[last - 4] = turn(last - 4)
-        scaled_of[last - 2] = scale_product(last - 2, product_of[last - 2])
+        second_parts(last - 2, product_of[last - 2])
         product_of[last - 1] = second_product(*quantised_of[last - 1], psum_z, "z")
         product_of[last] = second_product(*quantised_of[last], psum_z, "z")
         store(last - 4, turned_of[last - 4])
-        scaled_of[last - 1] = scale_product(last - 1, product_of[last - 1])
-        scaled_of[last] = scale_product(last, product_of[last])
+        second_parts(last - 1, product_of[last - 1])
+        second_parts(last, product_of[last])
         for block in (last - 2, last - 1, last):
-            second_leaky_relu(block, *scaled_of[block])
+            second_leaky_relu(block, product_of[block])
         for piece in (last - 3, last - 2, last - 1, last):
             turned_of[piece] = turn(piece, psum_z, "z")
         for piece in (last - 3, last - 2):

@@ -58,7 +58,7 @@ def tile_graph_gan_pa_t_kernel(tc, x, fe_w0, fe_b0, fe_w1, fe_b1, out):
     with ExitStack() as stack:
         keep = stack.enter_context(tc.tile_pool(name="keep", bufs=1))
         lines = stack.enter_context(tc.tile_pool(name="lines", bufs=8))
-        planes = stack.enter_context(tc.tile_pool(name="planes", bufs=4))
+        planes = stack.enter_context(tc.tile_pool(name="planes", bufs=6))
         hidden = stack.enter_context(tc.tile_pool(name="hidden", bufs=3))
         results = stack.enter_context(tc.tile_pool(name="results", bufs=5))
         operands = stack.enter_context(tc.tile_pool(name="operands", bufs=2))
@@ -327,26 +327,31 @@ def tile_graph_gan_pa_t_kernel(tc, x, fe_w0, fe_b0, fe_w1, fe_b1, out):
 
         linear_of, positive_of, maximum_of = {}, {}, {}
 
+        def vector_nodes_of(band):
+            return VECTOR_NODES if band < BLOCKS // BLOCKS_PER_BAND - 1 else 0
+
         def ordered(part, nodes):
             return part[:].rearrange("p (i q j) -> p q i j", i=nodes, q=SIDES)
 
         def second_parts(block, y_t):
             band, half = divmod(block, BLOCKS_PER_BAND)
+            vector_nodes = vector_nodes_of(band)
+            scalar_nodes = SIDE - vector_nodes
             if half == 0:
                 linear_of[band] = results.tile([P, SIDE * NODES], F32, name="linear")
-                positive_of[band] = results.tile([P, SCALAR_NODES * NODES], F32, name="positive")
+                positive_of[band] = results.tile([P, scalar_nodes * NODES], F32, name="positive")
             runs = slice(half * SQUARES_PER_BLOCK, (half + 1) * SQUARES_PER_BLOCK)
             squares = y_t[:].rearrange("p (s i j) -> p s i j", s=SQUARES_PER_BLOCK, i=SIDE)
+            linear = ordered(linear_of[band], SIDE)[:, runs, :, :]
+            if vector_nodes:
+                nc.scalar.activation(out=linear, in_=squares, func=IDENTITY, bias=b1_scaled[:], scale=ALPHA)
+            else:
+                nc.vector.tensor_scalar(
+                    out=linear, in0=squares, scalar1=ALPHA, scalar2=b1_scaled[:], op0=MULT, op1=ADD
+                )
             nc.scalar.activation(
-                out=ordered(linear_of[band], SIDE)[:, runs, :, :],
-                in_=squares,
-                func=IDENTITY,
-                bias=b1_scaled[:],
-                scale=ALPHA,
-            )
-            nc.scalar.activation(
-                out=ordered(positive_of[band], SCALAR_NODES)[:, runs, :, :],
-                in_=squares[:, :, VECTOR_NODES:, :],
+                out=ordered(positive_of[band], scalar_nodes)[:, runs, :, :],
+                in_=squares[:, :, vector_nodes:, :],
                 func=RELU,
                 bias=b1_rest[:],
                 scale=1.0 - ALPHA,
@@ -373,10 +378,10 @@ def tile_graph_gan_pa_t_kernel(tc, x, fe_w0, fe_b0, fe_w1, fe_b1, out):
             turned = pool.tile([P, PAIRS], F32, tag=tag)
             for g in range(PAIR_TILES):
                 first = (half * PAIR_TILES + g) * P
-                if first < VECTOR_NODES * NODES:
+                rest = first - vector_nodes_of(band) * NODES
+                if rest < 0:
                     columns = (maximum_of[band][:, first : first + P],)
                 else:
-                    rest = first - VECTOR_NODES * NODES
                     columns = (linear_of[band][:, first : first + P], positive_of[band][:, rest : rest + P])
                 for n, part in enumerate(columns):
                     nc.tensor.matmul(
@@ -431,6 +436,11 @@ def tile_graph_gan_pa_t_kernel(tc, x, fe_w0, fe_b0, fe_w1, fe_b1, out):
                 store(r - 5, turned_of[r - 5])
             if ft == 5 and 2 <= r:
                 product_of[r - 2] = second_product(*quantised_of[r - 2])
+            if ft == 7 and r == last:
+                second_parts(last - 2, product_of[last - 2])
+                second_leaky_relu(last - 2, product_of[last - 2])
+                turned_of[last - 4] = turn(last - 4)
+                store(last - 4, turned_of[last - 4])
             if ft == 7 and 1 <= r:
                 quantised_of[r - 1] = quantised_tiles()
                 quantise(e1_of[r - 1], quantised_of[r - 1], slice(0, PASSES))
@@ -448,21 +458,16 @@ def tile_graph_gan_pa_t_kernel(tc, x, fe_w0, fe_b0, fe_w1, fe_b1, out):
                 fill_rows(next_graph, operand_of[next_graph], 0, NODES)
 
         quantised_of[last] = quantised_tiles()
-        quantise(e1_of[last], quantised_of[last], slice(0, 1))
         regroup_last(planes_of[last, 1], e1_of[last], 1)
-        quantise(e1_of[last], quantised_of[last], slice(1, PASSES))
-        turned_of[last - 4] = turn(last - 4)
-        second_parts(last - 2, product_of[last - 2])
-        product_of[last - 1] = second_product(*quantised_of[last - 1], psum_z, "z")
-        product_of[last] = second_product(*quantised_of[last], psum_z, "z")
-        store(last - 4, turned_of[last - 4])
-        second_parts(last - 1, product_of[last - 1])
-        second_parts(last, product_of[last])
-        for block in (last - 2, last - 1, last):
-            second_leaky_relu(block, product_of[block])
-        for piece in (last - 3, last - 2, last - 1, last):
-            turned_of[piece] = turn(piece, psum_z, "z")
+        for c in range(PASSES):
+            quantise(e1_of[last], quantised_of[last], slice(c, c + 1))
         for piece in (last - 3, last - 2):
+            turned_of[piece] = turn(piece, psum_z, "z")
             store(piece, turned_of[piece])
+        for block in (last - 1, last):
+            product_of[block] = second_product(*quantised_of[block], psum_z, "z")
+            second_parts(block, product_of[block])
+        for piece in (last - 1, last):
+            turned_of[piece] = turn(piece, psum_z, "z")
         store(last - 1, turned_of[last - 1], copy=nc.vector.tensor_copy)
         store(last, turned_of[last], parts=2)

from contextlib import ExitStack

import concourse.mybir as mybir
from concourse.masks import make_identity

BF16 = mybir.dt.bfloat16
F32 = mybir.dt.float32
U32 = mybir.dt.uint32
U8 = mybir.dt.uint8
I32 = mybir.dt.int32
FP8X4 = mybir.dt.float8_e4m3fn_x4
ADD = mybir.AluOpType.add
MULT = mybir.AluOpType.mult
MAX = mybir.AluOpType.max
IDENTITY = mybir.ActivationFunctionType.Identity
RELU = mybir.ActivationFunctionType.Relu

P = 128
PACK = 4
K_PASS = P * PACK

GRAPHS, NODES, D_IN, HIDDEN, D_OUT = 4, 64, 512, 1024, 128
ROWS = GRAPHS * NODES
ROW_TILES = ROWS // P
HALVES = 2
PASSES = HIDDEN // K_PASS
FEATURE_TILES = HIDDEN // P
ALPHA = 0.2

SIDE = 16
SQUARE = SIDE * SIDE
SQUARES_PER_BLOCK = 2
PAIRS = SQUARES_PER_BLOCK * SQUARE
PAIR_TILES = PAIRS // P
BLOCKS_PER_BAND = 2
SIDES = NODES // SIDE
BLOCKS = ROWS * NODES // PAIRS
BLOCKS_PER_GRAPH = NODES * NODES // PAIRS
LAST_SCALAR_WORDS = 288
VECTOR_NODES = 8
SCALAR_NODES = SIDE - VECTOR_NODES

FLOPS = 2 * HALVES * ROWS * D_IN * HIDDEN + 2 * ROWS * NODES * HIDDEN * D_OUT


def side_by_side(copy, grouped, planes):
    copy(
        out=grouped.rearrange("p (g i) t -> p g t i", i=4),
        in_=planes.rearrange("p t (g i) -> p g t i", i=4),
    )


def tile_graph_gan_pa_t_kernel(tc, x, fe_w0, fe_b0, fe_w1, fe_b1, out):
    nc = tc.nc
    x_rows = x.flatten_outer_dims()
    out_rows = out.flatten_outer_dims()

    with ExitStack() as stack:
        keep = stack.enter_context(tc.tile_pool(name="keep", bufs=1))
        lines = stack.enter_context(tc.tile_pool(name="lines", bufs=8))
        planes = stack.enter_context(tc.tile_pool(name="planes", bufs=6))
        hidden = stack.enter_context(tc.tile_pool(name="hidden", bufs=3))
        results = stack.enter_context(tc.tile_pool(name="results", bufs=5))
        operands = stack.enter_context(tc.tile_pool(name="operands", bufs=2))
        psum_z = stack.enter_context(tc.psum_pool(name="psum_z", bufs=5))
        psum_out = stack.enter_context(tc.psum_pool(name="psum_out", bufs=2))
        psum_turn = stack.enter_context(tc.psum_pool(name="psum_turn", bufs=1))

        stack.enter_context(
            tc.manual_schedule(
                engines={
                    mybir.EngineType.PE,
                    mybir.EngineType.Activation,
                    mybir.EngineType.DVE,
                    mybir.EngineType.Pool,
                }
            )
        )

        identity_f32 = keep.tile([P, P], F32)
        make_identity(nc, identity_f32[:])
        b0_raw = keep.tile([P, PASSES, PACK], BF16)
        nc.scalar.dma_start(out=b0_raw[:], in_=fe_b0.rearrange("(c p t) -> p c t", p=P, t=PACK))
        b1_raw = keep.tile([P, 1], BF16)
        nc.scalar.dma_start(out=b1_raw[:], in_=fe_b1.rearrange("(p o) -> p o", o=1))
        warm = keep.tile([P, 1], F32)
        nc.gpsimd.memset(warm[:], 0.0)
        nc.scalar.activation(out=warm[:], in_=warm[:], func=IDENTITY, bias=0.0, scale=1.0)

        x_sb = keep.tile([P, ROW_TILES, D_IN], BF16)
        for r in range(ROW_TILES):
            nc.sync.dma_start(out=x_sb[:, r, :], in_=x_rows[r * P : (r + 1) * P, :])
        w0_planes = keep.tile([P, PASSES, HALVES, PACK, K_PASS], BF16)
        for c in range(PASSES):
            for h in range(HALVES):
                nc.sync.dma_start(
                    out=w0_planes[:, c, h, :, :],
                    in_=fe_w0[h * D_IN : (h + 1) * D_IN, c * K_PASS : (c + 1) * K_PASS].rearrange(
                        "(p t) f -> p t f", p=P
                    ),
                )
        w1_planes = keep.tile([P, PASSES, PACK, D_OUT], BF16)
        nc.sync.dma_start(
            out=w1_planes[:], in_=fe_w1.rearrange("(c p t) n -> p c t n", t=PACK, p=P)
        )

        x_codes = keep.tile([P, ROWS], U32, align_bytes=64)
        x_scales = keep.tile([P, ROWS], U8, align_bytes=64)
        nc.gpsimd.memset(x_scales[:].bitcast(I32), 0)
        x_grouped = keep.tile([P, ROWS, PACK], BF16, align_bytes=64)

        def quantise_x(r):
            tile_rows = slice(r * P, (r + 1) * P)
            nc.vector.quantize_mx(
                out=x_codes[:, tile_rows].bitcast(FP8X4),
                scales=x_scales[:, tile_rows],
                in_=x_grouped[:, tile_rows, :].rearrange("p r t -> p (r t)"),
            )

        def turn_x(r):
            x_words = x_sb[:, r, :].bitcast(F32)
            bank = psum_z.tile([P, PAIRS], F32, tag="z")
            x_t = bank[:, 0 : 2 * P].rearrange("p (e r) -> p e r", e=2)
            for e in range(2):
                nc.tensor.transpose(x_t[:, e, :], x_words[:, e::2], identity_f32[:])
            tile_rows = slice(r * P, (r + 1) * P)
            nc.scalar.copy(
                out=x_grouped[:, tile_rows, :].rearrange("p r t -> p (r t)").bitcast(F32),
                in_=x_t.rearrange("p e r -> p r e"),
            )

        def pair_operands(graph):
            rows = slice(graph * NODES, (graph + 1) * NODES)
            codes_i = operands.tile([P, NODES, SIDE], U32, align_bytes=64)
            scales_i = operands.tile([P, NODES, SIDE], U8, align_bytes=64)
            codes_j = operands.tile([P, SIDES, SIDE, SIDE], U32, align_bytes=64)
            scales_j = operands.tile([P, SIDES, SIDE, SIDE], U8, align_bytes=64)
            codes = x_codes[:, rows].bitcast(I32).rearrange("p (q j) -> p q j", q=SIDES)
            if graph == 0:
                nc.vector.tensor_copy(
                    out=codes_j[:].bitcast(I32), in_=codes.unsqueeze(2).to_broadcast([P, SIDES, SIDE, SIDE])
                )
            else:
                for q in range(SIDES):
                    nc.sync.dma_start(
                        out=codes_j[:, q, :, :].bitcast(I32),
                        in_=codes[:, q, :].unsqueeze(1).to_broadcast([P, SIDE, SIDE]),
                    )
            nc.vector.tensor_copy(
                out=scales_j[:]
                .rearrange("p q i j -> p (q i j)")
                .bitcast(I32)
                .rearrange("p (q i w) -> p q i w", q=SIDES, i=SIDE),
                in_=x_scales[:, rows]
                .bitcast(I32)
                .rearrange("p (q w) -> p q w", q=SIDES)
                .unsqueeze(2)
                .to_broadcast([P, SIDES, SIDE, SIDE // 4]),
            )
            return codes_i, scales_i, codes_j, scales_j

        bytes_4 = keep.tile([P, ROWS, 4], U8, align_bytes=64)

        def widen_scales(first, last):
            for n in range(4):
                nc.vector.tensor_copy(out=bytes_4[:, first:last, n], in_=x_scales[:, first:last])

        def fill_rows(graph, operand, first, last):
            codes_i, scales_i = operand[:2]
            count = last - first
            rows = slice(graph * NODES + first, graph * NODES + last)
            nc.vector.tensor_copy(
                out=codes_i[:, first:last, :].bitcast(I32),
                in_=x_codes[:, rows].bitcast(I32).unsqueeze(2).to_broadcast([P, count, SIDE]),
            )
            words_4 = bytes_4[:, rows, :].rearrange("p i n -> p (i n)").bitcast(I32)
            nc.vector.tensor_copy(
                out=scales_i[:, first:last, :]
                .rearrange("p i j -> p (i j)")
                .bitcast(I32)
                .rearrange("p (i w) -> p i w", i=count),
                in_=words_4.unsqueeze(2).to_broadcast([P, count, SIDE // 4]),
            )

        biases = keep.tile([P, FEATURE_TILES], F32)
        nc.gpsimd.tensor_copy(out=biases[:], in_=b0_raw[:].rearrange("p c t -> p (c t)"))
        biases_scaled = keep.tile([P, FEATURE_TILES], F32)
        nc.gpsimd.tensor_scalar(
            out=biases_scaled[:], in0=biases[:], scalar1=ALPHA, scalar2=0.0, op0=MULT, op1=ADD
        )
        b1_tile = keep.tile([P, 1], F32)
        nc.gpsimd.tensor_copy(out=b1_tile[:], in_=b1_raw[:])
        b1 = b1_tile[:]
        b1_scaled = keep.tile([P, 1], F32)
        nc.gpsimd.tensor_scalar(out=b1_scaled[:], in0=b1, scalar1=ALPHA, scalar2=0.0, op0=MULT, op1=ADD)
        b1_rest = keep.tile([P, 1], F32)
        nc.gpsimd.tensor_scalar(out=b1_rest[:], in0=b1, scalar1=1.0 - ALPHA, scalar2=0.0, op0=MULT, op1=ADD)

        w0_grouped = keep.tile([P, HALVES, HIDDEN, PACK], BF16, align_bytes=64)
        w0_codes = keep.tile([P, HALVES, HIDDEN], U32, align_bytes=64)
        w0_scales = keep.tile([P, HALVES, HIDDEN], U8, align_bytes=64)

        def group_w0(copy, c, h):
            f_cols = slice(c * K_PASS, (c + 1) * K_PASS)
            copy(
                out=w0_grouped[:, h, f_cols, :].rearrange("p (t m) k -> p m t k", t=PACK),
                in_=w0_planes[:, c, h, :, :].rearrange("p k (m t) -> p m t k", t=PACK),
            )

        def quantise_w0(c, h):
            f_cols = slice(c * K_PASS, (c + 1) * K_PASS)
            nc.vector.quantize_mx(
                out=w0_codes[:, h, f_cols].bitcast(FP8X4),
                scales=w0_scales[:, h, f_cols],
                in_=w0_grouped[:, h, f_cols, :].rearrange("p f t -> p (f t)"),
            )

        for r in range(ROW_TILES):
            turn_x(r)
        group_w0(nc.vector.tensor_copy, 0, 0)
        group_w0(nc.scalar.copy, 0, 1)
        quantise_x(0)
        operand_of = {0: pair_operands(0)}
        widen_scales(0, SIDE)
        fill_rows(0, operand_of[0], 0, SIDE)
        quantise_w0(0, 0)
        quantise_w0(0, 1)
        group_w0(nc.vector.tensor_copy, 1, 0)
        group_w0(nc.scalar.copy, 1, 1)
        quantise_w0(1, 0)
        quantise_w0(1, 1)
        quantise_x(1)

        w1_grouped = keep.tile([P, PASSES, D_OUT, PACK], BF16, align_bytes=64)
        w1_codes = keep.tile([P, PASSES, D_OUT], U32, align_bytes=64)
        w1_scales = keep.tile([P, PASSES, D_OUT], U8, align_bytes=64)

        def group_w1():
            for c in range(PASSES):
                side_by_side(nc.scalar.copy, w1_grouped[:, c, :, :], w1_planes[:, c, :, :])

        def quantise_w1():
            nc.vector.quantize_mx(
                out=w1_codes[:].rearrange("p c n -> p (c n)").bitcast(FP8X4),
                scales=w1_scales[:].rearrange("p c n -> p (c n)"),
                in_=w1_grouped[:].rearrange("p c n t -> p (c n t)"),
            )

        def first_layer(block, ft, operand, plane):
            codes_i, scales_i, codes_j, scales_j = operand
            band, half = divmod(block % BLOCKS_PER_GRAPH, BLOCKS_PER_BAND)
            i_rows = slice(band * SIDE, (band + 1) * SIDE)
            tile_cols = slice(ft * P, (ft + 1) * P)
            bank = psum_z.tile([P, PAIRS], F32, tag="z")
            for s in range(SQUARES_PER_BLOCK):
                square = bank[:, s * SQUARE : (s + 1) * SQUARE]
                q = half * SQUARES_PER_BLOCK + s
                nc.tensor.matmul_mx(
                    out=square,
                    lhsT=w0_codes[:, 0, tile_cols].bitcast(FP8X4),
                    lhsT_scale=w0_scales[:, 0, tile_cols],
                    rhs=codes_i[:, i_rows, :].rearrange("p i j -> p (i j)").bitcast(FP8X4),
                    rhs_scale=scales_i[:, i_rows, :].rearrange("p i j -> p (i j)"),
                    start=True,
                    stop=False,
                )
                nc.tensor.matmul_mx(
                    out=square,
                    lhsT=w0_codes[:, 1, tile_cols].bitcast(FP8X4),
                    lhsT_scale=w0_scales[:, 1, tile_cols],
                    rhs=codes_j[:, q, :, :].rearrange("p i j -> p (i j)").bitcast(FP8X4),
                    rhs_scale=scales_j[:, q, :, :].rearrange("p i j -> p (i j)"),
                    start=False,
                    stop=True,
                )
            low = lines.tile([P, PAIRS], F32)
            nc.scalar.activation(
                out=low[:], in_=bank[:], func=IDENTITY, bias=biases_scaled[:, ft : ft + 1], scale=ALPHA
            )
            nc.vector.scalar_tensor_tensor(
                out=plane, in0=bank[:], scalar=biases[:, ft : ft + 1], in1=low[:], op0=ADD, op1=MAX
            )

        def regroup(e1_planes, e1, c):
            nc.gpsimd.tensor_scalar(
                out=e1[:, c, :, :].rearrange("p (g i) t -> p g t i", i=4),
                in0=e1_planes[:].rearrange("p t (g i) -> p g t i", i=4),
                scalar1=1.0,
                scalar2=0.0,
                op0=MULT,
                op1=ADD,
            )

        def regroup_last(e1_planes, e1, c):
            cut = PAIRS - LAST_SCALAR_WORDS
            side_by_side(nc.scalar.copy, e1[:, c, cut:, :], e1_planes[:, :, cut:])
            nc.vector.tensor_copy(
                out=e1[:, c, :cut, :], in_=e1_planes[:, :, :cut].rearrange("p t w -> p w t")
            )

        def quantised_tiles():
            codes = hidden.tile([P, PASSES, PAIRS], U32, align_bytes=64)
            scales = hidden.tile([P, PASSES, PAIRS], U8, align_bytes=64)
            return codes, scales

        def quantise(e1, quantised, run):
            codes, scales = quantised
            nc.vector.quantize_mx(
                out=codes[:, run, :].rearrange("p c w -> p (c w)").bitcast(FP8X4),
                scales=scales[:, run, :].rearrange("p c w -> p (c w)"),
                in_=e1[:, run, :, :].rearrange("p c w t -> p (c w t)"),
            )

        def second_product(codes, scales, pool=psum_out, tag="y"):
            y_t = pool.tile([P, PAIRS], F32, tag=tag)
            for c in range(PASSES):
                nc.tensor.matmul_mx(
                    out=y_t[:],
                    lhsT=w1_codes[:, c, :].bitcast(FP8X4),
                    lhsT_scale=w1_scales[:, c, :],
                    rhs=codes[:, c, :].bitcast(FP8X4),
                    rhs_scale=scales[:, c, :],
                    start=(c == 0),
                    stop=(c == PASSES - 1),
                )
            return y_t

        linear_of, positive_of, maximum_of = {}, {}, {}

        def vector_nodes_of(band):
            return VECTOR_NODES if band < BLOCKS // BLOCKS_PER_BAND - 1 else 0

        def ordered(part, nodes):
            return part[:].rearrange("p (i q j) -> p q i j", i=nodes, q=SIDES)

        def second_parts(block, y_t):
            band, half = divmod(block, BLOCKS_PER_BAND)
            vector_nodes = vector_nodes_of(band)
            scalar_nodes = SIDE - vector_nodes
            if half == 0:
                linear_of[band] = results.tile([P, SIDE * NODES], F32, name="linear")
                positive_of[band] = results.tile([P, scalar_nodes * NODES], F32, name="positive")
            runs = slice(half * SQUARES_PER_BLOCK, (half + 1) * SQUARES_PER_BLOCK)
            squares = y_t[:].rearrange("p (s i j) -> p s i j", s=SQUARES_PER_BLOCK, i=SIDE)
            linear = ordered(linear_of[band], SIDE)[:, runs, :, :]
            if vector_nodes:
                nc.scalar.activation(out=linear, in_=squares, func=IDENTITY, bias=b1_scaled[:], scale=ALPHA)
            else:
                nc.vector.tensor_scalar(
                    out=linear, in0=squares, scalar1=ALPHA, scalar2=b1_scaled[:], op0=MULT, op1=ADD
                )
            nc.scalar.activation(
                out=ordered(positive_of[band], scalar_nodes)[:, runs, :, :],
                in_=squares[:, :, vector_nodes:, :],
                func=RELU,
                bias=b1_rest[:],
                scale=1.0 - ALPHA,
            )

        def second_leaky_relu(block, y_t):
            band, half = divmod(block, BLOCKS_PER_BAND)
            if half == 0:
                maximum_of[band] = results.tile([P, VECTOR_NODES * NODES], F32, name="maximum")
            squares = y_t[:].rearrange("p (s i j) -> p s i j", s=SQUARES_PER_BLOCK, i=SIDE)
            for s in range(SQUARES_PER_BLOCK):
                q = half * SQUARES_PER_BLOCK + s
                nc.vector.scalar_tensor_tensor(
                    out=ordered(maximum_of[band], VECTOR_NODES)[:, q, :, :],
                    in0=squares[:, s, :VECTOR_NODES, :],
                    scalar=b1,
                    in1=ordered(linear_of[band], SIDE)[:, q, :VECTOR_NODES, :],
                    op0=ADD,
                    op1=MAX,
                )

        def turn(piece, pool=psum_turn, tag="turned"):
            band, half = divmod(piece, BLOCKS_PER_BAND)
            turned = pool.tile([P, PAIRS], F32, tag=tag)
            for g in range(PAIR_TILES):
                first = (half * PAIR_TILES + g) * P
                rest = first - vector_nodes_of(band) * NODES
                if rest < 0:
                    columns = (maximum_of[band][:, first : first + P],)
                else:
                    columns = (linear_of[band][:, first : first + P], positive_of[band][:, rest : rest + P])
                for n, part in enumerate(columns):
                    nc.tensor.matmul(
                        turned[:, g * P : (g + 1) * P],
                        lhsT=part,
                        rhs=identity_f32[:],
                        is_transpose=True,
                        start=(n == 0),
                        stop=(n == len(columns) - 1),
                    )
            return turned

        def store(piece, turned, parts=1, copy=nc.scalar.copy):
            result = results.tile([P, PAIR_TILES, D_OUT], F32)
            tiles = PAIR_TILES // parts
            for g in range(0, PAIR_TILES, tiles):
                copy(
                    out=result[:, g : g + tiles, :].rearrange("p g n -> p (g n)"),
                    in_=turned[:, g * P : (g + tiles) * P],
                )
                first = piece * PAIRS + g * P
                nc.sync.dma_start(
                    out=out_rows[first : first + tiles * P, :].rearrange("(g p) n -> p g n", p=P),
                    in_=result[:, g : g + tiles, :],
                )

        last = BLOCKS - 1
        e1_of, planes_of, quantised_of, product_of = {}, {}, {}, {}
        turned_of = {}
        order = [(0, 0)]
        for r in range(BLOCKS):
            order.extend((r, ft) for ft in range(1, FEATURE_TILES - 1))
            order.extend([(r + 1, 0)] if r < last else [])
            order.append((r, FEATURE_TILES - 1))
        for r, ft in order:
            operand = operand_of[r // BLOCKS_PER_GRAPH]
            c, t = divmod(ft, PACK)
            if ft == 0:
                e1_of[r] = hidden.tile([P, PASSES, PAIRS, PACK], BF16, align_bytes=64, name="e1")
            if t == 0:
                planes_of[r, c] = planes.tile([P, PACK, PAIRS], BF16, name="e1_planes")
            first_layer(r, ft, operand, planes_of[r, c][:, t, :])
            if t == PACK - 1 and (r, c) != (last, PASSES - 1):
                regroup(planes_of[r, c], e1_of[r], c)
            if ft == 1 and 3 <= r:
                second_parts(r - 3, product_of[r - 3])
            if ft == 1 and 5 <= r:
                turned_of[r - 5] = turn(r - 5)
            if ft == 4 and 3 <= r:
                second_leaky_relu(r - 3, product_of[r - 3])
            if ft == 4 and 5 <= r:
                store(r - 5, turned_of[r - 5])
            if ft == 5 and 2 <= r:
                product_of[r - 2] = second_product(*quantised_of[r - 2])
            if ft == 7 and r == last:
                second_parts(last - 2, product_of[last - 2])
                second_leaky_relu(last - 2, product_of[last - 2])
                turned_of[last - 4] = turn(last - 4)
                store(last - 4, turned_of[last - 4])
            if ft == 7 and 1 <= r:
                quantised_of[r - 1] = quantised_tiles()
                quantise(e1_of[r - 1], quantised_of[r - 1], slice(0, PASSES))
            if r == 0 and ft == 0:
                widen_scales(SIDE, NODES)
                fill_rows(0, operand, SIDE, NODES)
            if r == 0 and ft == 4:
                group_w1()
            if r == 0 and ft == 7:
                quantise_w1()
                widen_scales(NODES, ROWS)
            if ft == 7 and r + 2 < BLOCKS and (r + 2) % BLOCKS_PER_GRAPH == 0:
                next_graph = (r + 2) // BLOCKS_PER_GRAPH
                operand_of[next_graph] = pair_operands(next_graph)
                fill_rows(next_graph, operand_of[next_graph], 0, NODES)

        quantised_of[last] = quantised_tiles()
        regroup_last(planes_of[last, 1], e1_of[last], 1)
        for c in range(PASSES):
            quantise(e1_of[last], quantised_of[last], slice(c, c + 1))
        for piece in (last - 3, last - 2):
            turned_of[piece] = turn(piece, psum_z, "z")
            store(piece, turned_of[piece])
        for block in (last - 1, last):
            product_of[block] = second_product(*quantised_of[block], psum_z, "z")
            second_parts(block, product_of[block])
        for piece in (last - 1, last):
            turned_of[piece] = turn(piece, psum_z, "z")
        store(last - 1, turned_of[last - 1], copy=nc.vector.tensor_copy)
        store(last, turned_of[last], parts=2)
